import numpy as np
import ml_dtypes


def mxq(x, axis, fmt="e4m3"):
    dtype, down = {"e4m3": (ml_dtypes.float8_e4m3fn, 7), "e5m2": (ml_dtypes.float8_e5m2, 14)}[fmt]
    v = np.moveaxis(np.asarray(x, np.float32).astype(ml_dtypes.bfloat16).astype(np.float64), axis, -1)
    blocks = v.reshape(v.shape[:-1] + (-1, 32))
    amax = np.abs(blocks).max(-1, keepdims=True)
    byte = np.maximum(np.where(amax > 0, np.frexp(amax)[1] - 1 + 127, 0) - down, 1)
    scale = np.exp2(byte - 127.0)
    codes = (blocks / scale).astype(np.float32).astype(dtype).astype(np.float64)
    return np.moveaxis((codes * scale).reshape(v.shape), -1, axis)


WIDE = False


def mx_kscale(k):
    if not WIDE:
        return np.ones(k)
    levels = np.array([10, -10, 5, -5, 0])
    if k % 512:
        return np.exp2(np.random.permutation(np.resize(levels, k // 32))).repeat(32)
    a = np.empty((k // 512, 16))
    for p in range(k // 512):
        a[p, :8] = np.random.permutation(np.resize(levels, 8))
        for g in range(8):
            far = levels[np.abs(levels - a[p, g]) >= 10]
            a[p, g + 8] = far[np.random.randint(len(far))]
    return np.exp2(a.ravel()).repeat(32)


BF16 = ml_dtypes.bfloat16


def bf(x):
    return np.asarray(x, np.float32).astype(BF16)


def f64(x):
    return np.asarray(x).astype(np.float64)


B, C, O, H, W, KH, KW, PAD = 4, 512, 256, 32, 32, 3, 3, 1
C_CURV = 0.01
EPS = 1e-7


def artanh(z):
    return 0.5 * np.log((1.0 + z) / (1.0 - z))


def log0(y):
    sqc = np.sqrt(C_CURV)
    n = np.maximum(np.sqrt((y * y).sum(-1, keepdims=True)), EPS)
    return artanh(np.clip(sqc * n, 0.0, 1.0 - 1e-6)) * y / (sqc * n)


def exp0(v):
    sqc = np.sqrt(C_CURV)
    n = np.maximum(np.sqrt((v * v).sum(-1, keepdims=True)), EPS)
    return np.tanh(sqc * n) * v / (sqc * n)


def setup_inputs():
    s = mx_kscale(C)
    rho = np.sqrt(np.mean(s * s))
    raw = np.random.uniform(0.0, 1.0, (B, C, H, W)) * s[None, :, None, None]
    r = np.random.uniform(0.2, 0.85, (B, 1, H, W))
    x = raw / np.sqrt((raw * raw).sum(1, keepdims=True)) * r / np.sqrt(C_CURV)
    return {"x": bf(x),
            "Wk": bf(np.random.standard_normal((KH * KW, O, C)) * 2.1 / np.sqrt(KH * KW * O) * rho / s),
            "bias": bf(np.random.standard_normal(O) * 5.0 / np.sqrt(O))}


def reference(x, Wk, bias):
    Hout, Wout = H + 2 * PAD - KH + 1, W + 2 * PAD - KW + 1
    u = log0(np.moveaxis(f64(x), 1, -1)).reshape(B * H * W, C)
    w = f64(Wk).transpose(2, 0, 1).reshape(C, KH * KW * O)
    y = mxq(u, 1, "e4m3") @ mxq(w, 0, "e4m3")
    yp = np.pad(y.reshape(B, H, W, KH * KW, O), ((0, 0), (PAD, PAD), (PAD, PAD), (0, 0), (0, 0)))
    v = sum(yp[:, i:i + Hout, j:j + Wout, KW * i + j, :] for i in range(KH) for j in range(KW))
    v = np.maximum(v + f64(bias), 0.0)
    out = exp0(v)
    return np.transpose(out, (0, 3, 1, 2))

@@ -1,0 +1,354 @@
+from contextlib import ExitStack
+
+import concourse.mybir as mybir
+from concourse.masks import make_identity
+
+FP8X4 = mybir.dt.float8_e4m3fn_x4
+BF16 = mybir.dt.bfloat16
+F32 = mybir.dt.float32
+I32 = mybir.dt.int32
+U32 = mybir.dt.uint32
+U8 = mybir.dt.uint8
+ALU = mybir.AluOpType
+ACT = mybir.ActivationFunctionType
+
+P = 128
+B, C, O, H, W = 4, 512, 256, 32, 32
+FLOPS = 2 * B * H * W * C * 9 * O
+ZMAX = 1.0 - 1e-6
+ROWS = 8
+NCH = 8
+PADW = (H + 2) * 64
+ACC_BUFS, TP_BUFS, BC_BUFS = 3, 2, 3
+EARLY_RELU = 0
+EARLY_COPY = 0
+
+
+def tile_pvconv2d_t_kernel(tc, x, Wk, bias, out):
+    nc = tc.nc
+    with ExitStack() as ctx:
+        ctx.enter_context(tc.manual_schedule())
+        const = ctx.enter_context(tc.tile_pool(name="const", bufs=1))
+        upool = ctx.enter_context(tc.tile_pool(name="upool", bufs=2))
+        junkp = ctx.enter_context(tc.tile_pool(name="junkp", bufs=2))
+        rpool = ctx.enter_context(tc.tile_pool(name="rpool", bufs=12))
+        opool = ctx.enter_context(tc.tile_pool(name="opool", bufs=6))
+        tp = ctx.enter_context(tc.psum_pool(name="tp", bufs=TP_BUFS))
+        bc = ctx.enter_context(tc.psum_pool(name="bc", bufs=BC_BUFS))
+        accp = ctx.enter_context(tc.psum_pool(name="accp", bufs=ACC_BUFS))
+
+        ident_f = const.tile([P, P], F32, name="ident_f")
+        make_identity(nc, ident_f[:])
+        ident_b = const.tile([P, P], BF16, name="ident_b")
+        make_identity(nc, ident_b[:])
+        ones1 = const.tile([P, 1], F32, name="ones1")
+        nc.vector.memset(ones1[:], 1.0)
+        mhalf4 = const.tile([P, 4], F32, name="mhalf4")
+        nc.vector.memset(mhalf4[:], -0.5)
+        zeros = const.tile([P, 16, 4], BF16, name="zeros")
+        nc.vector.memset(zeros[:], 0.0)
+        warm = const.tile([P, 1], F32, name="warm")
+        nc.scalar.activation(out=warm[:], in_=ones1[:], func=ACT.Ln)
+        btile = const.tile([P, P], BF16, name="btile")
+        nc.vector.memset(btile[:], 0.0)
+
+        codes = [[const.tile([P, PADW], U32, name="codes%d%d" % (j, bp), align_bytes=64) for bp in range(2)] for j in range(3)]
+        planes = [[const.tile([P, PADW], U8, name="planes%d%d" % (j, bp), align_bytes=64) for bp in range(2)] for j in range(3)]
+        ul = [const.tile([P, 16, 128], BF16, name="ul%d" % k, align_bytes=64) for k in range(2)]
+        ur = [const.tile([P, 16, 128], BF16, name="ur%d" % k, align_bytes=64) for k in range(2)]
+        for k in range(2):
+            nc.vector.memset(ul[k][:, :, 0:4], 0.0)
+            nc.scalar.copy(out=ur[k][:, :, 124:128], in_=zeros[:])
+        for j in range(3):
+            for bp in range(2):
+                for lo in (0, PADW - 64):
+                    nc.vector.memset(codes[j][bp][:, lo:lo + 64].bitcast(I32), 0)
+                    nc.vector.memset(planes[j][bp][:, lo:lo + 64].bitcast(I32), 0)
+
+        names = ["n2", "y4", "z2", "zc", "la", "lb", "rzh", "dd", "gg", "m2", "y2o", "zm", "th", "rzo", "tf"]
+        sm = dict((nm, const.tile([P, 4 * NCH], F32, name="sm_" + nm)) for nm in names)
+
+        def s4(nm, c):
+            return sm[nm][:, 4 * c:4 * c + 4]
+
+        xs = [const.tile([P, 4, H * W], BF16, name="xs%d" % b) for b in range(B)]
+        w_sb = const.tile([P, 18, C], BF16, name="w_sb")
+        wk_v = Wk.rearrange("k (h p) c -> p (k h) c", p=P)
+
+        def load_x_half(b, hh):
+            xv = x[b].rearrange("(q t) h w -> q t (h w)", t=4)
+            nc.sync.dma_start(out=xs[b][:, :, hh * 512:(hh + 1) * 512], in_=xv[:, :, hh * 512:(hh + 1) * 512])
+
+        def load_w(k3):
+            nc.sync.dma_start(out=w_sb[:, 6 * k3:6 * k3 + 6, :], in_=wk_v[:, 6 * k3:6 * k3 + 6, :])
+
+        nc.scalar.dma_start(out=btile[0:2, :], in_=bias.rearrange("(h o) -> h o", h=2))
+        load_x_half(0, 0)
+        load_x_half(1, 0)
+        load_w(0)
+        load_w(1)
+        load_w(2)
+        load_x_half(0, 1)
+        load_x_half(1, 1)
+        load_x_half(2, 0)
+        load_x_half(3, 0)
+        load_x_half(2, 1)
+        load_x_half(3, 1)
+
+        wg = const.tile([P, 18, P, 4], BF16, name="wg", align_bytes=64)
+        wc = const.tile([P, 18 * P], U32, name="wc", align_bytes=64)
+        ws = const.tile([P, 18 * P], U8, name="ws", align_bytes=64)
+        w_f = w_sb[:].bitcast(F32)
+        wg_f = wg[:].bitcast(F32)
+
+        def w_transpose(k):
+            wt = accp.tile([P, 2, 2, P], F32, name="wt", tag="acc")
+            for bl in range(2):
+                for u in range(2):
+                    nc.tensor.transpose(wt[:, bl, u, :], w_f[:, 2 * k + bl, u:2 * P:2], ident_f[:])
+            if k < 3:
+                nc.vector.tensor_copy(out=wg_f[:, 2 * k:2 * k + 2, :, :], in_=wt[:].rearrange("p b u o -> p b o u"))
+            else:
+                nc.scalar.copy(out=wg_f[:, 2 * k:2 * k + 2, :, :], in_=wt[:].rearrange("p b u o -> p b o u"))
+
+        def w_quant(k):
+            nc.vector.quantize_mx(
+                out=wc[:, 256 * k:256 * k + 256].bitcast(FP8X4),
+                scales=ws[:, 256 * k:256 * k + 256],
+                in_=wg[:, 2 * k:2 * k + 2, :, :].rearrange("p b o t -> p (b o t)"),
+            )
+
+        def w_group(ks):
+            for n, k in enumerate(ks):
+                w_transpose(k)
+                if n > 0:
+                    w_quant(ks[n - 1])
+            w_quant(ks[-1])
+
+        def x_norm(c, b2):
+            bp, hq = divmod(c, 4)
+            xf = xs[2 * bp + b2][:].bitcast(F32)
+            xt = tp.tile([P, 4, P], F32, name="xt", tag="tp")
+            for t in range(4):
+                nc.tensor.transpose(xt[:, t, :], xf[:, t, hq * P:(hq + 1) * P], ident_f[:])
+            xv = xt[:].bitcast(BF16).rearrange("p t (q par) -> p par t q", par=2)
+            for par in range(2):
+                junk = junkp.tile([P, 4, P], BF16, name="junk")
+                col = 4 * c + 2 * b2 + par
+                nc.scalar.activation(out=junk[:], in_=xv[:, par], func=ACT.Square,
+                                     accum_out=sm["n2"][:, col:col + 1])
+
+        def chain_in_a(c):
+            nc.gpsimd.tensor_scalar(out=s4("y4", c), in0=s4("n2", c), scalar1=0.04, scalar2=4e-16,
+                                    op0=ALU.mult, op1=ALU.max)
+            nc.gpsimd.tensor_tensor(out=s4("rzh", c), in0=s4("y4", c), in1=mhalf4[:], op=ALU.pow)
+            nc.gpsimd.tensor_tensor(out=s4("z2", c), in0=s4("y4", c), in1=s4("rzh", c), op=ALU.mult)
+            nc.gpsimd.tensor_scalar(out=s4("zc", c), in0=s4("z2", c), scalar1=0.5, scalar2=ZMAX,
+                                    op0=ALU.mult, op1=ALU.min)
+
+        def chain_in_b(c):
+            nc.scalar.activation(out=s4("la", c), in_=s4("zc", c), func=ACT.Ln, bias=ones1[:], scale=1.0)
+            nc.scalar.activation(out=s4("lb", c), in_=s4("zc", c), func=ACT.Ln, bias=ones1[:], scale=-1.0)
+            nc.gpsimd.tensor_tensor(out=s4("dd", c), in0=s4("la", c), in1=s4("lb", c), op=ALU.subtract)
+            nc.gpsimd.tensor_tensor(out=s4("gg", c), in0=s4("dd", c), in1=s4("rzh", c), op=ALU.mult)
+
+        g_banks = {}
+
+        def g_bcast(c):
+            gb = bc.tile([P, 4, P], F32, name="gb", tag="bc")
+            for k in range(4):
+                nc.tensor.transpose(gb[:, k, :], sm["gg"][:, 4 * c + k:4 * c + k + 1].to_broadcast([P, P]), ident_f[:])
+            g_banks[c] = gb
+
+        def u_stage(c, fill):
+            bp, hq = divmod(c, 4)
+            gb = g_banks[c]
+            uc = upool.tile([P, ROWS, 2, W, 4], BF16, name="uc", align_bytes=64)
+            for b2 in range(2):
+                in0 = xs[2 * bp + b2][:, :, hq * 256:(hq + 1) * 256].rearrange(
+                    "p t (h w2 par) -> p h w2 par t", h=ROWS, w2=16, par=2)
+                in1 = gb[:, 2 * b2:2 * b2 + 2, :].rearrange("p par (h w2) -> p h w2 par", h=ROWS)
+                in1 = in1.unsqueeze(4).to_broadcast([P, ROWS, 16, 2, 4])
+                o = uc[:, :, b2, :, :].rearrange("p h (w2 par) t -> p h w2 par t", par=2)
+                nc.vector.tensor_tensor(out=o, in0=in0, in1=in1, op=ALU.mult)
+            ucr = uc[:].rearrange("p h b w t -> p (h b) (w t)")
+            k = c % 2
+            lo = (ROWS * hq + 1) * 64
+            srcs = [ul[k][:].rearrange("p r c -> p (r c)"), uc[:].rearrange("p h b w t -> p (h b w t)"),
+                    ur[k][:].rearrange("p r c -> p (r c)")]
+
+            def quant(j):
+                nc.vector.quantize_mx(out=codes[j][bp][:, lo:lo + 512].bitcast(FP8X4),
+                                      scales=planes[j][bp][:, lo:lo + 512], in_=srcs[j])
+
+            if c >= EARLY_COPY:
+                nc.scalar.copy(out=ur[k][:, :, 0:124], in_=ucr[:, :, 4:128])
+            quant(1)
+            nc.vector.tensor_copy(out=ul[k][:, :, 4:128], in_=ucr[:, :, 0:124])
+            if c < EARLY_COPY:
+                nc.vector.tensor_copy(out=ur[k][:, :, 0:124], in_=ucr[:, :, 4:128])
+            for f in fill[0]:
+                f()
+            quant(0)
+            quant(2)
+            for f in fill[1]:
+                f()
+
+        accs = {}
+        r_tiles = {}
+
+        def mx_passes(s, half, i_list, first, last):
+            bp, hq = divmod(s, 4)
+            if first:
+                acc_new = accp.tile([P, 512], F32, name="acc", tag="acc")
+                accs[(s, half)] = acc_new
+            acc = accs[(s, half)]
+            todo = [(i, j) for j in (1, 0, 2) for i in i_list]
+            for n, (i, j) in enumerate(todo):
+                blk = 2 * (3 * i + j) + half
+                lo = (ROWS * hq + i) * 64
+                nc.tensor.matmul_mx(
+                    out=acc[:],
+                    lhsT=wc[:, blk * P:(blk + 1) * P].bitcast(FP8X4),
+                    lhsT_scale=ws[:, blk * P:(blk + 1) * P],
+                    rhs=codes[j][bp][:, lo:lo + 512].bitcast(FP8X4),
+                    rhs_scale=planes[j][bp][:, lo:lo + 512],
+                    start=(first and n == 0), stop=(last and n == len(todo) - 1),
+                )
+
+        def relu(s, half):
+            r = rpool.tile([P, 512], F32, name="r")
+            if s < EARLY_RELU:
+                nc.vector.tensor_scalar(out=r[:], in0=accs[(s, half)][:], scalar1=bias_sb[:, half:half + 1], scalar2=0.0,
+                                        op0=ALU.add, op1=ALU.max)
+            else:
+                nc.scalar.activation(out=r[:], in_=accs[(s, half)][:], func=ACT.Relu,
+                                     bias=bias_sb[:, half:half + 1], scale=1.0)
+            r_tiles[(s, half)] = r
+
+        def out_norm(s, pg):
+            rt = tp.tile([P, 2, 2, P], F32, name="rt", tag="tp")
+            for pl in range(2):
+                pb = 2 * pg + pl
+                for half in range(2):
+                    nc.tensor.transpose(rt[:, pl, half, :], r_tiles[(s, half)][:, pb * P:(pb + 1) * P], ident_f[:])
+            for pl in range(2):
+                junk = junkp.tile([P, 2, P], BF16, name="junk2")
+                col = 4 * s + 2 * pg + pl
+                nc.scalar.activation(out=junk[:], in_=rt[:, pl], func=ACT.Square,
+                                     accum_out=sm["m2"][:, col:col + 1])
+
+        def chain_out_a(s):
+            nc.gpsimd.tensor_scalar(out=s4("y2o", s), in0=s4("m2", s), scalar1=0.01, scalar2=1e-16,
+                                    op0=ALU.mult, op1=ALU.max)
+            nc.gpsimd.tensor_tensor(out=s4("rzo", s), in0=s4("y2o", s), in1=mhalf4[:], op=ALU.pow)
+            nc.gpsimd.tensor_tensor(out=s4("zm", s), in0=s4("y2o", s), in1=s4("rzo", s), op=ALU.mult)
+
+        def chain_out_b(s):
+            nc.scalar.activation(out=s4("th", s), in_=s4("zm", s), func=ACT.Tanh)
+            nc.gpsimd.tensor_tensor(out=s4("tf", s), in0=s4("th", s), in1=s4("rzo", s), op=ALU.mult)
+
+        t_banks = {}
+
+        def t_bcast(s):
+            tb = bc.tile([P, 4, P], F32, name="tb", tag="bc")
+            for k in range(4):
+                nc.tensor.transpose(tb[:, k, :], sm["tf"][:, 4 * s + k:4 * s + k + 1].to_broadcast([P, P]), ident_f[:])
+            t_banks[s] = tb
+
+        def finish(s, half):
+            bp, hq = divmod(s, 4)
+            tv = t_banks[s][:].rearrange("p k (a b w) -> p (k a) b w", a=2, b=2)
+            ob = opool.tile([P, 2, ROWS, W], F32, name="ob")
+            rv = r_tiles[(s, half)][:].rearrange("p (h b w) -> p h b w", h=ROWS, b=2)
+            nc.vector.tensor_tensor(out=ob[:].rearrange("p b h w -> p h b w"), in0=rv, in1=tv, op=ALU.mult)
+            nc.sync.dma_start(
+                out=out[2 * bp:2 * bp + 2, half * P:(half + 1) * P, ROWS * hq:ROWS * hq + ROWS, :].rearrange(
+                    "b p h w -> p b (h w)"),
+                in_=ob[:].rearrange("p b h w -> p b (h w)"),
+            )
+
+        def nothing():
+            return None
+
+        def finisher(s, half):
+            if 0 <= s < NCH:
+                return lambda: finish(s, half)
+            return nothing
+
+        def x_chunk(c):
+            x_norm(c, 0)
+            if c > 0:
+                chain_in_b(c - 1)
+            x_norm(c, 1)
+            chain_in_a(c)
+
+        bt = tp.tile([P, P], BF16, name="bt", tag="tp")
+        nc.tensor.transpose(bt[:], btile[:], ident_b[:])
+        bias_sb = const.tile([P, 2], F32, name="bias_sb")
+        nc.vector.tensor_copy(out=bias_sb[:], in_=bt[:, 0:2])
+        x_chunk(0)
+        x_chunk(1)
+        w_group([0, 1, 2])
+        g_bcast(0)
+        for k in (3, 4, 5):
+            w_transpose(k)
+        chain_in_b(1)
+        for k in (6, 7, 8):
+            w_transpose(k)
+        u_stage(0, [[lambda: w_quant(3), lambda: w_quant(4)], [lambda: w_quant(5)]])
+        g_bcast(1)
+        x_norm(2, 0)
+        x_norm(2, 1)
+        chain_in_a(2)
+        for k in (6, 7, 8):
+            w_quant(k)
+
+        def tanh_step(s):
+            return s + 3 if s < 4 else s + 2
+
+        def tile_norm(s):
+            out_norm(s, 0)
+            out_norm(s, 1)
+            chain_out_a(s)
+
+        for c in range(NCH + 4):
+            if 1 <= c <= NCH and (c - 1) % 4 < 3:
+                for half in range(2):
+                    mx_passes(c - 1, half, [2], False, True)
+                    relu(c - 1, half)
+            ready = [s for s in range(NCH) if tanh_step(s) == c]
+            mid = (False) and c < NCH
+            if c < NCH:
+                for s in ready:
+                    chain_out_b(s)
+                closes = (c % 4 == 3)
+                mx_passes(c, 0, [0, 1, 2] if closes else [0, 1], True, closes)
+                if closes:
+                    relu(c, 0)
+                if mid:
+                    tile_norm(c - 1)
+                if 2 * c + 3 < NCH:
+                    x_chunk(2 * c + 3)
+                mx_passes(c, 1, [0, 1, 2] if closes else [0, 1], True, closes)
+                if closes:
+                    relu(c, 1)
+            fins = [finisher(s, half) for s in range(NCH) if tanh_step(s) + 1 == c for half in range(2)]
+            if c + 1 < NCH:
+                u_stage(c + 1, [fins[0:1], fins[1:]])
+            else:
+                for f in fins:
+                    f()
+            if c == 2:
+                chain_in_b(7)
+            if 0 <= c - 1 < NCH and not mid:
+                tile_norm(c - 1)
+            if c >= NCH:
+                for s in ready:
+                    chain_out_b(s)
+            if c + 2 < NCH:
+                g_bcast(c + 2)
+            for s in ready:
+                t_bcast(s)
+            if 2 * c + 4 < NCH:
+                x_chunk(2 * c + 4)

@@ -21,7 +21,6 @@ NCH = 8
 PADW = (H + 2) * 64
 ACC_BUFS, TP_BUFS, BC_BUFS = 3, 2, 3
 EARLY_RELU = 0
-EARLY_COPY = 0
 
 
 def tile_pvconv2d_t_kernel(tc, x, Wk, bias, out):
@@ -45,8 +44,6 @@ def tile_pvconv2d_t_kernel(tc, x, Wk, bias, out):
         nc.vector.memset(ones1[:], 1.0)
         mhalf4 = const.tile([P, 4], F32, name="mhalf4")
         nc.vector.memset(mhalf4[:], -0.5)
-        zeros = const.tile([P, 16, 4], BF16, name="zeros")
-        nc.vector.memset(zeros[:], 0.0)
         warm = const.tile([P, 1], F32, name="warm")
         nc.scalar.activation(out=warm[:], in_=ones1[:], func=ACT.Ln)
         btile = const.tile([P, P], BF16, name="btile")
@@ -54,16 +51,14 @@ def tile_pvconv2d_t_kernel(tc, x, Wk, bias, out):
 
         codes = [[const.tile([P, PADW], U32, name="codes%d%d" % (j, bp), align_bytes=64) for bp in range(2)] for j in range(3)]
         planes = [[const.tile([P, PADW], U8, name="planes%d%d" % (j, bp), align_bytes=64) for bp in range(2)] for j in range(3)]
-        ul = [const.tile([P, 16, 128], BF16, name="ul%d" % k, align_bytes=64) for k in range(2)]
-        ur = [const.tile([P, 16, 128], BF16, name="ur%d" % k, align_bytes=64) for k in range(2)]
-        for k in range(2):
-            nc.vector.memset(ul[k][:, :, 0:4], 0.0)
-            nc.scalar.copy(out=ur[k][:, :, 124:128], in_=zeros[:])
-        for j in range(3):
-            for bp in range(2):
+        for bp in range(2):
+            for j in range(3):
+                nc.vector.memset(planes[j][bp][:].bitcast(I32), 0)
                 for lo in (0, PADW - 64):
                     nc.vector.memset(codes[j][bp][:, lo:lo + 64].bitcast(I32), 0)
-                    nc.vector.memset(planes[j][bp][:, lo:lo + 64].bitcast(I32), 0)
+            for j, w in ((0, 0), (2, W - 1)):
+                border = codes[j][bp][:].bitcast(I32).rearrange("p (r w) -> p r w", w=W)
+                nc.vector.memset(border[:, :, w:w + 1], 0)
 
         names = ["n2", "y4", "z2", "zc", "la", "lb", "rzh", "dd", "gg", "m2", "y2o", "zm", "th", "rzo", "tf"]
         sm = dict((nm, const.tile([P, 4 * NCH], F32, name="sm_" + nm)) for nm in names)
@@ -171,26 +166,20 @@ def tile_pvconv2d_t_kernel(tc, x, Wk, bias, out):
                 in1 = in1.unsqueeze(4).to_broadcast([P, ROWS, 16, 2, 4])
                 o = uc[:, :, b2, :, :].rearrange("p h (w2 par) t -> p h w2 par t", par=2)
                 nc.vector.tensor_tensor(out=o, in0=in0, in1=in1, op=ALU.mult)
-            ucr = uc[:].rearrange("p h b w t -> p (h b) (w t)")
-            k = c % 2
             lo = (ROWS * hq + 1) * 64
-            srcs = [ul[k][:].rearrange("p r c -> p (r c)"), uc[:].rearrange("p h b w t -> p (h b w t)"),
-                    ur[k][:].rearrange("p r c -> p (r c)")]
-
-            def quant(j):
-                nc.vector.quantize_mx(out=codes[j][bp][:, lo:lo + 512].bitcast(FP8X4),
-                                      scales=planes[j][bp][:, lo:lo + 512], in_=srcs[j])
-
-            if c >= EARLY_COPY:
-                nc.scalar.copy(out=ur[k][:, :, 0:124], in_=ucr[:, :, 4:128])
-            quant(1)
-            nc.vector.tensor_copy(out=ul[k][:, :, 4:128], in_=ucr[:, :, 0:124])
-            if c < EARLY_COPY:
-                nc.vector.tensor_copy(out=ur[k][:, :, 0:124], in_=ucr[:, :, 4:128])
+            nc.vector.quantize_mx(out=codes[1][bp][:, lo:lo + 512].bitcast(FP8X4),
+                                  scales=planes[1][bp][:, lo:lo + 512],
+                                  in_=uc[:].rearrange("p h b w t -> p (h b w t)"))
             for f in fill[0]:
                 f()
-            quant(0)
-            quant(2)
+
+            def rows_of(t):
+                return t[:, lo:lo + 512].rearrange("p (r w) -> p r w", w=W)
+
+            for j, dst, src in ((0, slice(1, W), slice(0, W - 1)), (2, slice(0, W - 1), slice(1, W))):
+                nc.vector.tensor_copy(out=rows_of(codes[j][bp][:].bitcast(I32))[:, :, dst],
+                                      in_=rows_of(codes[1][bp][:].bitcast(I32))[:, :, src])
+                nc.vector.tensor_copy(out=rows_of(planes[j][bp])[:, :, dst], in_=rows_of(planes[1][bp])[:, :, src])
             for f in fill[1]:
                 f()
 

@@ -19,8 +19,8 @@ ZMAX = 1.0 - 1e-6
 ROWS = 8
 NCH = 8
 PADW = (H + 2) * 64
-ACC_BUFS, TP_BUFS, BC_BUFS = 3, 2, 3
-EARLY_RELU = 0
+GRAM = (0, 1, 7)
+LAST = NCH - 1
 
 
 def tile_pvconv2d_t_kernel(tc, x, Wk, bias, out):
@@ -32,9 +32,36 @@ def tile_pvconv2d_t_kernel(tc, x, Wk, bias, out):
         junkp = ctx.enter_context(tc.tile_pool(name="junkp", bufs=2))
         rpool = ctx.enter_context(tc.tile_pool(name="rpool", bufs=12))
         opool = ctx.enter_context(tc.tile_pool(name="opool", bufs=6))
-        tp = ctx.enter_context(tc.psum_pool(name="tp", bufs=TP_BUFS))
-        bc = ctx.enter_context(tc.psum_pool(name="bc", bufs=BC_BUFS))
-        accp = ctx.enter_context(tc.psum_pool(name="accp", bufs=ACC_BUFS))
+        tp = ctx.enter_context(tc.psum_pool(name="tp", bufs=2))
+        bc = ctx.enter_context(tc.psum_pool(name="bc", bufs=3))
+        accp = ctx.enter_context(tc.psum_pool(name="accp", bufs=3))
+
+        xs = [const.tile([P, 4, H * W], BF16, name="xs%d" % b) for b in range(B)]
+        w_sb = const.tile([P, 18, C], BF16, name="w_sb")
+        wk_v = Wk.rearrange("k (h p) c -> p (k h) c", p=P)
+        btile = const.tile([P, P], BF16, name="btile")
+
+        def load_x(b, lo, hi):
+            xv = x[b].rearrange("(q t) h w -> q t (h w)", t=4)
+            nc.sync.dma_start(out=xs[b][:, :, lo * W:hi * W], in_=xv[:, :, lo * W:hi * W])
+
+        def load_w(k3):
+            nc.sync.dma_start(out=w_sb[:, 6 * k3:6 * k3 + 6, :], in_=wk_v[:, 6 * k3:6 * k3 + 6, :])
+
+        nc.vector.memset(btile[:], 0.0)
+        load_x(0, 0, 8)
+        load_x(1, 0, 8)
+        load_x(0, 8, 16)
+        load_x(1, 8, 16)
+        load_w(0)
+        load_w(1)
+        nc.scalar.dma_start(out=btile[0:2, :], in_=bias.rearrange("(h o) -> h o", h=2))
+        load_x(0, 16, 32)
+        load_x(1, 16, 32)
+        load_w(2)
+        for half in range(2):
+            load_x(2, 16 * half, 16 * half + 16)
+            load_x(3, 16 * half, 16 * half + 16)
 
         ident_f = const.tile([P, P], F32, name="ident_f")
         make_identity(nc, ident_f[:])
@@ -42,18 +69,17 @@ def tile_pvconv2d_t_kernel(tc, x, Wk, bias, out):
         make_identity(nc, ident_b[:])
         ones1 = const.tile([P, 1], F32, name="ones1")
         nc.vector.memset(ones1[:], 1.0)
-        mhalf4 = const.tile([P, 4], F32, name="mhalf4")
-        nc.vector.memset(mhalf4[:], -0.5)
+        mhalf8 = const.tile([P, 8], F32, name="mhalf8")
+        nc.vector.memset(mhalf8[:], -0.5)
         warm = const.tile([P, 1], F32, name="warm")
         nc.scalar.activation(out=warm[:], in_=ones1[:], func=ACT.Ln)
-        btile = const.tile([P, P], BF16, name="btile")
-        nc.vector.memset(btile[:], 0.0)
 
         codes = [[const.tile([P, PADW], U32, name="codes%d%d" % (j, bp), align_bytes=64) for bp in range(2)] for j in range(3)]
         planes = [[const.tile([P, PADW], U8, name="planes%d%d" % (j, bp), align_bytes=64) for bp in range(2)] for j in range(3)]
-        for bp in range(2):
+
+        def clear_borders(bp):
             for j in range(3):
-                nc.vector.memset(planes[j][bp][:].bitcast(I32), 0)
+                nc.gpsimd.memset(planes[j][bp][:].bitcast(I32), 0)
                 for lo in (0, PADW - 64):
                     nc.vector.memset(codes[j][bp][:, lo:lo + 64].bitcast(I32), 0)
             for j, w in ((0, 0), (2, W - 1)):
@@ -63,32 +89,8 @@ def tile_pvconv2d_t_kernel(tc, x, Wk, bias, out):
         names = ["n2", "y4", "z2", "zc", "la", "lb", "rzh", "dd", "gg", "m2", "y2o", "zm", "th", "rzo", "tf"]
         sm = dict((nm, const.tile([P, 4 * NCH], F32, name="sm_" + nm)) for nm in names)
 
-        def s4(nm, c):
-            return sm[nm][:, 4 * c:4 * c + 4]
-
-        xs = [const.tile([P, 4, H * W], BF16, name="xs%d" % b) for b in range(B)]
-        w_sb = const.tile([P, 18, C], BF16, name="w_sb")
-        wk_v = Wk.rearrange("k (h p) c -> p (k h) c", p=P)
-
-        def load_x_half(b, hh):
-            xv = x[b].rearrange("(q t) h w -> q t (h w)", t=4)
-            nc.sync.dma_start(out=xs[b][:, :, hh * 512:(hh + 1) * 512], in_=xv[:, :, hh * 512:(hh + 1) * 512])
-
-        def load_w(k3):
-            nc.sync.dma_start(out=w_sb[:, 6 * k3:6 * k3 + 6, :], in_=wk_v[:, 6 * k3:6 * k3 + 6, :])
-
-        nc.scalar.dma_start(out=btile[0:2, :], in_=bias.rearrange("(h o) -> h o", h=2))
-        load_x_half(0, 0)
-        load_x_half(1, 0)
-        load_w(0)
-        load_w(1)
-        load_w(2)
-        load_x_half(0, 1)
-        load_x_half(1, 1)
-        load_x_half(2, 0)
-        load_x_half(3, 0)
-        load_x_half(2, 1)
-        load_x_half(3, 1)
+        def cols(nm, lo, n):
+            return sm[nm][:, lo:lo + n]
 
         wg = const.tile([P, 18, P, 4], BF16, name="wg", align_bytes=64)
         wc = const.tile([P, 18 * P], U32, name="wc", align_bytes=64)
@@ -96,15 +98,16 @@ def tile_pvconv2d_t_kernel(tc, x, Wk, bias, out):
         w_f = w_sb[:].bitcast(F32)
         wg_f = wg[:].bitcast(F32)
 
-        def w_transpose(k):
+        def w_transpose(k, eng):
             wt = accp.tile([P, 2, 2, P], F32, name="wt", tag="acc")
             for bl in range(2):
                 for u in range(2):
                     nc.tensor.transpose(wt[:, bl, u, :], w_f[:, 2 * k + bl, u:2 * P:2], ident_f[:])
-            if k < 3:
-                nc.vector.tensor_copy(out=wg_f[:, 2 * k:2 * k + 2, :, :], in_=wt[:].rearrange("p b u o -> p b o u"))
+            src = wt[:].rearrange("p b u o -> p b o u")
+            if eng is nc.vector:
+                nc.vector.tensor_copy(out=wg_f[:, 2 * k:2 * k + 2, :, :], in_=src)
             else:
-                nc.scalar.copy(out=wg_f[:, 2 * k:2 * k + 2, :, :], in_=wt[:].rearrange("p b u o -> p b o u"))
+                nc.scalar.copy(out=wg_f[:, 2 * k:2 * k + 2, :, :], in_=src)
 
         def w_quant(k):
             nc.vector.quantize_mx(
@@ -113,41 +116,63 @@ def tile_pvconv2d_t_kernel(tc, x, Wk, bias, out):
                 in_=wg[:, 2 * k:2 * k + 2, :, :].rearrange("p b o t -> p (b o t)"),
             )
 
-        def w_group(ks):
-            for n, k in enumerate(ks):
-                w_transpose(k)
-                if n > 0:
-                    w_quant(ks[n - 1])
-            w_quant(ks[-1])
-
-        def x_norm(c, b2):
+        def x_gram(c):
             bp, hq = divmod(c, 4)
-            xf = xs[2 * bp + b2][:].bitcast(F32)
-            xt = tp.tile([P, 4, P], F32, name="xt", tag="tp")
-            for t in range(4):
-                nc.tensor.transpose(xt[:, t, :], xf[:, t, hq * P:(hq + 1) * P], ident_f[:])
-            xv = xt[:].bitcast(BF16).rearrange("p t (q par) -> p par t q", par=2)
-            for par in range(2):
-                junk = junkp.tile([P, 4, P], BF16, name="junk")
-                col = 4 * c + 2 * b2 + par
-                nc.scalar.activation(out=junk[:], in_=xv[:, par], func=ACT.Square,
-                                     accum_out=sm["n2"][:, col:col + 1])
+            pool, tag = (tp, "tp") if c < 2 else (bc, "bc")
+            gm = pool.tile([P, 4, P], F32, name="gm", tag=tag)
+            for k in range(4):
+                b2, q = divmod(k, 2)
+                lo = hq * 256 + q * P
+                for t in range(4):
+                    px = xs[2 * bp + b2][:, t, lo:lo + P]
+                    nc.tensor.matmul(gm[:, k, :], lhsT=px, rhs=px, start=(t == 0), stop=(t == 3))
+            for k in range(4):
+                junk = junkp.tile([P, P], F32, name="junkg")
+                nc.vector.scalar_tensor_tensor(out=junk[:], in0=gm[:, k, :], scalar=1.0, in1=ident_f[:],
+                                               op0=ALU.mult, op1=ALU.mult,
+                                               accum_out=sm["n2"][:, 4 * c + k:4 * c + k + 1])
 
-        def chain_in_a(c):
-            nc.gpsimd.tensor_scalar(out=s4("y4", c), in0=s4("n2", c), scalar1=0.04, scalar2=4e-16,
-                                    op0=ALU.mult, op1=ALU.max)
-            nc.gpsimd.tensor_tensor(out=s4("rzh", c), in0=s4("y4", c), in1=mhalf4[:], op=ALU.pow)
-            nc.gpsimd.tensor_tensor(out=s4("z2", c), in0=s4("y4", c), in1=s4("rzh", c), op=ALU.mult)
-            nc.gpsimd.tensor_scalar(out=s4("zc", c), in0=s4("z2", c), scalar1=0.5, scalar2=ZMAX,
-                                    op0=ALU.mult, op1=ALU.min)
+        x_banks = {}
 
-        def chain_in_b(c):
-            nc.scalar.activation(out=s4("la", c), in_=s4("zc", c), func=ACT.Ln, bias=ones1[:], scale=1.0)
-            nc.scalar.activation(out=s4("lb", c), in_=s4("zc", c), func=ACT.Ln, bias=ones1[:], scale=-1.0)
-            nc.gpsimd.tensor_tensor(out=s4("dd", c), in0=s4("la", c), in1=s4("lb", c), op=ALU.subtract)
-            nc.gpsimd.tensor_tensor(out=s4("gg", c), in0=s4("dd", c), in1=s4("rzh", c), op=ALU.mult)
+        def x_words(c):
+            bp, hq = divmod(c, 4)
+            for b2 in range(2):
+                xf = xs[2 * bp + b2][:].bitcast(F32)
+                xt = tp.tile([P, 4, P], F32, name="xt", tag="tp")
+                for t in range(4):
+                    nc.tensor.transpose(xt[:, t, :], xf[:, t, hq * P:(hq + 1) * P], ident_f[:])
+                x_banks[(c, b2)] = xt
+
+        def x_squares(c):
+            for b2 in range(2):
+                xv = x_banks[(c, b2)][:].bitcast(BF16).rearrange("p t (q par) -> p par t q", par=2)
+                for par in range(2):
+                    junk = junkp.tile([P, 4, P], BF16, name="junk")
+                    col = 4 * c + 2 * b2 + par
+                    nc.scalar.activation(out=junk[:], in_=xv[:, par], func=ACT.Square,
+                                         accum_out=sm["n2"][:, col:col + 1])
+
+        def chain_in_a(c, eng):
+            lo = 4 * c
+            eng.tensor_scalar(out=cols("y4", lo, 4), in0=cols("n2", lo, 4), scalar1=0.04, scalar2=4e-16,
+                              op0=ALU.mult, op1=ALU.max)
+            nc.gpsimd.tensor_tensor(out=cols("rzh", lo, 4), in0=cols("y4", lo, 4), in1=mhalf8[:, 0:4], op=ALU.pow)
+
+        def chain_in_b(c, eng):
+            lo = 4 * c
+            eng.tensor_tensor(out=cols("z2", lo, 4), in0=cols("y4", lo, 4), in1=cols("rzh", lo, 4), op=ALU.mult)
+            eng.tensor_scalar(out=cols("zc", lo, 4), in0=cols("z2", lo, 4), scalar1=0.5, scalar2=ZMAX,
+                              op0=ALU.mult, op1=ALU.min)
+
+        def chain_in_c(c, eng):
+            lo = 4 * c
+            nc.scalar.activation(out=cols("la", lo, 4), in_=cols("zc", lo, 4), func=ACT.Ln, bias=ones1[:], scale=1.0)
+            nc.scalar.activation(out=cols("lb", lo, 4), in_=cols("zc", lo, 4), func=ACT.Ln, bias=ones1[:], scale=-1.0)
+            eng.tensor_tensor(out=cols("dd", lo, 4), in0=cols("la", lo, 4), in1=cols("lb", lo, 4), op=ALU.subtract)
+            eng.tensor_tensor(out=cols("gg", lo, 4), in0=cols("dd", lo, 4), in1=cols("rzh", lo, 4), op=ALU.mult)
 
         g_banks = {}
+        u_tiles = {}
 
         def g_bcast(c):
             gb = bc.tile([P, 4, P], F32, name="gb", tag="bc")
@@ -155,189 +180,273 @@ def tile_pvconv2d_t_kernel(tc, x, Wk, bias, out):
                 nc.tensor.transpose(gb[:, k, :], sm["gg"][:, 4 * c + k:4 * c + k + 1].to_broadcast([P, P]), ident_f[:])
             g_banks[c] = gb
 
-        def u_stage(c, fill):
+        def u_mult(c, b2):
             bp, hq = divmod(c, 4)
-            gb = g_banks[c]
-            uc = upool.tile([P, ROWS, 2, W, 4], BF16, name="uc", align_bytes=64)
-            for b2 in range(2):
-                in0 = xs[2 * bp + b2][:, :, hq * 256:(hq + 1) * 256].rearrange(
-                    "p t (h w2 par) -> p h w2 par t", h=ROWS, w2=16, par=2)
-                in1 = gb[:, 2 * b2:2 * b2 + 2, :].rearrange("p par (h w2) -> p h w2 par", h=ROWS)
-                in1 = in1.unsqueeze(4).to_broadcast([P, ROWS, 16, 2, 4])
-                o = uc[:, :, b2, :, :].rearrange("p h (w2 par) t -> p h w2 par t", par=2)
-                nc.vector.tensor_tensor(out=o, in0=in0, in1=in1, op=ALU.mult)
+            if b2 == 0:
+                uc_new = upool.tile([P, ROWS, 2, W, 4], BF16, name="uc", align_bytes=64)
+                u_tiles[c] = uc_new
+            gv = g_banks[c][:, 2 * b2:2 * b2 + 2, :]
+            xv = xs[2 * bp + b2][:, :, hq * 256:(hq + 1) * 256]
+            uv = u_tiles[c][:, :, b2, :, :]
+            if c in GRAM:
+                in0 = xv.rearrange("p t (h w) -> p h w t", w=W)
+                in1 = gv.rearrange("p q (h w) -> p (q h) w", w=W).unsqueeze(3).to_broadcast([P, ROWS, W, 4])
+                nc.vector.tensor_tensor(out=uv, in0=in0, in1=in1, op=ALU.mult)
+            else:
+                in0 = xv.rearrange("p t (h w2 par) -> p h w2 par t", h=ROWS, par=2)
+                in1 = gv.rearrange("p par (h w2) -> p h w2 par", h=ROWS).unsqueeze(4).to_broadcast([P, ROWS, 16, 2, 4])
+                nc.vector.tensor_tensor(out=uv.rearrange("p h (w2 par) t -> p h w2 par t", par=2), in0=in0, in1=in1,
+                                        op=ALU.mult)
+
+        def u_quant(c):
+            bp, hq = divmod(c, 4)
             lo = (ROWS * hq + 1) * 64
             nc.vector.quantize_mx(out=codes[1][bp][:, lo:lo + 512].bitcast(FP8X4),
                                   scales=planes[1][bp][:, lo:lo + 512],
-                                  in_=uc[:].rearrange("p h b w t -> p (h b w t)"))
-            for f in fill[0]:
-                f()
+                                  in_=u_tiles[c][:].rearrange("p h b w t -> p (h b w t)"))
+
+        def u_move(c, j):
+            bp, hq = divmod(c, 4)
+            lo = (ROWS * hq + 1) * 64
 
             def rows_of(t):
                 return t[:, lo:lo + 512].rearrange("p (r w) -> p r w", w=W)
 
-            for j, dst, src in ((0, slice(1, W), slice(0, W - 1)), (2, slice(0, W - 1), slice(1, W))):
-                nc.vector.tensor_copy(out=rows_of(codes[j][bp][:].bitcast(I32))[:, :, dst],
-                                      in_=rows_of(codes[1][bp][:].bitcast(I32))[:, :, src])
-                nc.vector.tensor_copy(out=rows_of(planes[j][bp])[:, :, dst], in_=rows_of(planes[1][bp])[:, :, src])
-            for f in fill[1]:
-                f()
+            dst, src = (slice(1, W), slice(0, W - 1)) if j == 0 else (slice(0, W - 1), slice(1, W))
+            nc.vector.tensor_copy(out=rows_of(codes[j][bp][:].bitcast(I32))[:, :, dst],
+                                  in_=rows_of(codes[1][bp][:].bitcast(I32))[:, :, src])
+            nc.vector.tensor_copy(out=rows_of(planes[j][bp])[:, :, dst], in_=rows_of(planes[1][bp])[:, :, src])
 
         accs = {}
         r_tiles = {}
 
-        def mx_passes(s, half, i_list, first, last):
+        def mx_passes(s, half, i_list, first, last, lo=0, n=512):
             bp, hq = divmod(s, 4)
-            if first:
+            if first and lo == 0:
                 acc_new = accp.tile([P, 512], F32, name="acc", tag="acc")
                 accs[(s, half)] = acc_new
             acc = accs[(s, half)]
             todo = [(i, j) for j in (1, 0, 2) for i in i_list]
-            for n, (i, j) in enumerate(todo):
+            for m, (i, j) in enumerate(todo):
                 blk = 2 * (3 * i + j) + half
-                lo = (ROWS * hq + i) * 64
+                px = (ROWS * hq + i) * 64 + lo
                 nc.tensor.matmul_mx(
-                    out=acc[:],
+                    out=acc[:, lo:lo + n],
                     lhsT=wc[:, blk * P:(blk + 1) * P].bitcast(FP8X4),
                     lhsT_scale=ws[:, blk * P:(blk + 1) * P],
-                    rhs=codes[j][bp][:, lo:lo + 512].bitcast(FP8X4),
-                    rhs_scale=planes[j][bp][:, lo:lo + 512],
-                    start=(first and n == 0), stop=(last and n == len(todo) - 1),
+                    rhs=codes[j][bp][:, px:px + n].bitcast(FP8X4),
+                    rhs_scale=planes[j][bp][:, px:px + n],
+                    start=(first and m == 0), stop=(last and m == len(todo) - 1),
                 )
 
-        def relu(s, half):
-            r = rpool.tile([P, 512], F32, name="r")
-            if s < EARLY_RELU:
-                nc.vector.tensor_scalar(out=r[:], in0=accs[(s, half)][:], scalar1=bias_sb[:, half:half + 1], scalar2=0.0,
+        def relu(s, half, eng, lo=0, n=512):
+            if lo == 0:
+                r_new = rpool.tile([P, 512], F32, name="r")
+                r_tiles[(s, half)] = r_new
+            dst, src = r_tiles[(s, half)][:, lo:lo + n], accs[(s, half)][:, lo:lo + n]
+            if eng is nc.vector:
+                nc.vector.tensor_scalar(out=dst, in0=src, scalar1=bias_sb[:, half:half + 1], scalar2=0.0,
                                         op0=ALU.add, op1=ALU.max)
             else:
-                nc.scalar.activation(out=r[:], in_=accs[(s, half)][:], func=ACT.Relu,
-                                     bias=bias_sb[:, half:half + 1], scale=1.0)
-            r_tiles[(s, half)] = r
+                nc.scalar.activation(out=dst, in_=src, func=ACT.Relu, bias=bias_sb[:, half:half + 1], scale=1.0)
 
-        def out_norm(s, pg):
+        r_banks = {}
+
+        def r_words(s, pg):
             rt = tp.tile([P, 2, 2, P], F32, name="rt", tag="tp")
             for pl in range(2):
                 pb = 2 * pg + pl
                 for half in range(2):
                     nc.tensor.transpose(rt[:, pl, half, :], r_tiles[(s, half)][:, pb * P:(pb + 1) * P], ident_f[:])
+            r_banks[(s, pg)] = rt
+
+        def r_squares(s, pg):
             for pl in range(2):
                 junk = junkp.tile([P, 2, P], BF16, name="junk2")
                 col = 4 * s + 2 * pg + pl
-                nc.scalar.activation(out=junk[:], in_=rt[:, pl], func=ACT.Square,
+                nc.scalar.activation(out=junk[:], in_=r_banks[(s, pg)][:, pl], func=ACT.Square,
                                      accum_out=sm["m2"][:, col:col + 1])
 
-        def chain_out_a(s):
-            nc.gpsimd.tensor_scalar(out=s4("y2o", s), in0=s4("m2", s), scalar1=0.01, scalar2=1e-16,
-                                    op0=ALU.mult, op1=ALU.max)
-            nc.gpsimd.tensor_tensor(out=s4("rzo", s), in0=s4("y2o", s), in1=mhalf4[:], op=ALU.pow)
-            nc.gpsimd.tensor_tensor(out=s4("zm", s), in0=s4("y2o", s), in1=s4("rzo", s), op=ALU.mult)
+        def chain_out_a(s, eng, lo=0, n=4):
+            lo = 4 * s + lo
+            eng.tensor_scalar(out=cols("y2o", lo, n), in0=cols("m2", lo, n), scalar1=0.01, scalar2=1e-16,
+                              op0=ALU.mult, op1=ALU.max)
+            nc.gpsimd.tensor_tensor(out=cols("rzo", lo, n), in0=cols("y2o", lo, n), in1=mhalf8[:, 0:n], op=ALU.pow)
+            eng.tensor_tensor(out=cols("zm", lo, n), in0=cols("y2o", lo, n), in1=cols("rzo", lo, n), op=ALU.mult)
 
-        def chain_out_b(s):
-            nc.scalar.activation(out=s4("th", s), in_=s4("zm", s), func=ACT.Tanh)
-            nc.gpsimd.tensor_tensor(out=s4("tf", s), in0=s4("th", s), in1=s4("rzo", s), op=ALU.mult)
+        def chain_out_b(s, eng, lo=0, n=4):
+            lo = 4 * s + lo
+            nc.scalar.activation(out=cols("th", lo, n), in_=cols("zm", lo, n), func=ACT.Tanh)
+            eng.tensor_tensor(out=cols("tf", lo, n), in0=cols("th", lo, n), in1=cols("rzo", lo, n), op=ALU.mult)
 
         t_banks = {}
 
-        def t_bcast(s):
-            tb = bc.tile([P, 4, P], F32, name="tb", tag="bc")
-            for k in range(4):
-                nc.tensor.transpose(tb[:, k, :], sm["tf"][:, 4 * s + k:4 * s + k + 1].to_broadcast([P, P]), ident_f[:])
-            t_banks[s] = tb
+        def t_bcast(s, lo=0, n=4):
+            if lo == 0:
+                tb_new = bc.tile([P, 4, P], F32, name="tb", tag="bc")
+                t_banks[s] = tb_new
+            for k in range(lo, lo + n):
+                nc.tensor.transpose(t_banks[s][:, k, :], sm["tf"][:, 4 * s + k:4 * s + k + 1].to_broadcast([P, P]),
+                                    ident_f[:])
 
-        def finish(s, half):
+        def finish(s, half, lo=0, n=4):
             bp, hq = divmod(s, 4)
-            tv = t_banks[s][:].rearrange("p k (a b w) -> p (k a) b w", a=2, b=2)
-            ob = opool.tile([P, 2, ROWS, W], F32, name="ob")
-            rv = r_tiles[(s, half)][:].rearrange("p (h b w) -> p h b w", h=ROWS, b=2)
+            rows = 2 * n
+            tv = t_banks[s][:, lo:lo + n, :].rearrange("p k (a b w) -> p (k a) b w", a=2, b=2)
+            ob = opool.tile([P, 2, rows, W], F32, name="ob%d" % rows)
+            rv = r_tiles[(s, half)][:, lo * P:(lo + n) * P].rearrange("p (h b w) -> p h b w", h=rows, b=2)
             nc.vector.tensor_tensor(out=ob[:].rearrange("p b h w -> p h b w"), in0=rv, in1=tv, op=ALU.mult)
+            r0 = ROWS * hq + 2 * lo
             nc.sync.dma_start(
-                out=out[2 * bp:2 * bp + 2, half * P:(half + 1) * P, ROWS * hq:ROWS * hq + ROWS, :].rearrange(
-                    "b p h w -> p b (h w)"),
+                out=out[2 * bp:2 * bp + 2, half * P:(half + 1) * P, r0:r0 + rows, :].rearrange("b p h w -> p b (h w)"),
                 in_=ob[:].rearrange("p b h w -> p b (h w)"),
             )
 
-        def nothing():
-            return None
-
-        def finisher(s, half):
-            if 0 <= s < NCH:
-                return lambda: finish(s, half)
-            return nothing
-
-        def x_chunk(c):
-            x_norm(c, 0)
-            if c > 0:
-                chain_in_b(c - 1)
-            x_norm(c, 1)
-            chain_in_a(c)
-
-        bt = tp.tile([P, P], BF16, name="bt", tag="tp")
-        nc.tensor.transpose(bt[:], btile[:], ident_b[:])
         bias_sb = const.tile([P, 2], F32, name="bias_sb")
-        nc.vector.tensor_copy(out=bias_sb[:], in_=bt[:, 0:2])
-        x_chunk(0)
-        x_chunk(1)
-        w_group([0, 1, 2])
+
+        def bias_columns():
+            bt = bc.tile([P, P], BF16, name="bt", tag="bc")
+            nc.tensor.transpose(bt[:], btile[:], ident_b[:])
+            nc.vector.tensor_copy(out=bias_sb[:], in_=bt[:, 0:2])
+
+        def chain_in_ab(c, eng):
+            chain_in_a(c, eng)
+            chain_in_b(c, eng)
+
+        V, G = nc.vector, nc.gpsimd
+        clear_borders(0)
+        clear_borders(1)
+        x_gram(0)
+        chain_in_a(0, V)
+        x_gram(1)
+        chain_in_b(0, V)
+        chain_in_c(0, V)
+        chain_in_a(1, V)
+        for k in (0, 1, 2):
+            w_transpose(k, nc.scalar)
         g_bcast(0)
-        for k in (3, 4, 5):
-            w_transpose(k)
-        chain_in_b(1)
-        for k in (6, 7, 8):
-            w_transpose(k)
-        u_stage(0, [[lambda: w_quant(3), lambda: w_quant(4)], [lambda: w_quant(5)]])
+        w_quant(0)
+        w_quant(1)
+        chain_in_b(1, V)
+        chain_in_c(1, V)
+        w_quant(2)
+        for k in (4, 3, 5):
+            w_transpose(k, nc.scalar)
+        u_mult(0, 0)
+        u_mult(0, 1)
+        w_quant(4)
+        u_quant(0)
+        w_quant(3)
+        u_move(0, 0)
+        w_quant(5)
+        u_move(0, 2)
         g_bcast(1)
-        x_norm(2, 0)
-        x_norm(2, 1)
-        chain_in_a(2)
-        for k in (6, 7, 8):
-            w_quant(k)
+        bias_columns()
+        x_words(2)
+        x_squares(2)
+        chain_in_ab(2, G)
 
-        def tanh_step(s):
-            return s + 3 if s < 4 else s + 2
+        S = nc.scalar
 
-        def tile_norm(s):
-            out_norm(s, 0)
-            out_norm(s, 1)
-            chain_out_a(s)
+        def fin(s):
+            finish(s, 0)
+            finish(s, 1)
 
-        for c in range(NCH + 4):
-            if 1 <= c <= NCH and (c - 1) % 4 < 3:
+        def norm_in(n):
+            if n in GRAM:
+                x_gram(n)
+            else:
+                x_words(n)
+                x_squares(n)
+            chain_in_ab(n, G)
+
+        def norm_out(s, eng):
+            for pg in range(2):
+                r_words(s, pg)
+                r_squares(s, pg)
+            chain_out_a(s, eng)
+
+        scaled = {3: (0,), 4: (1, 2), 5: (3,), 6: (4,)}
+        for c in range(LAST):
+            whole = c % 4 == 3
+            taps = [0, 1, 2] if whole else [0, 1]
+            if c % 4 > 0:
                 for half in range(2):
                     mx_passes(c - 1, half, [2], False, True)
-                    relu(c - 1, half)
-            ready = [s for s in range(NCH) if tanh_step(s) == c]
-            mid = (False) and c < NCH
-            if c < NCH:
-                for s in ready:
-                    chain_out_b(s)
-                closes = (c % 4 == 3)
-                mx_passes(c, 0, [0, 1, 2] if closes else [0, 1], True, closes)
-                if closes:
-                    relu(c, 0)
-                if mid:
-                    tile_norm(c - 1)
-                if 2 * c + 3 < NCH:
-                    x_chunk(2 * c + 3)
-                mx_passes(c, 1, [0, 1, 2] if closes else [0, 1], True, closes)
-                if closes:
-                    relu(c, 1)
-            fins = [finisher(s, half) for s in range(NCH) if tanh_step(s) + 1 == c for half in range(2)]
-            if c + 1 < NCH:
-                u_stage(c + 1, [fins[0:1], fins[1:]])
-            else:
-                for f in fins:
-                    f()
-            if c == 2:
-                chain_in_b(7)
-            if 0 <= c - 1 < NCH and not mid:
-                tile_norm(c - 1)
-            if c >= NCH:
-                for s in ready:
-                    chain_out_b(s)
-            if c + 2 < NCH:
-                g_bcast(c + 2)
-            for s in ready:
+                    relu(c - 1, half, S)
+            if c == 3:
+                chain_in_c(7, G)
+                chain_out_b(0, G)
+                chain_out_b(1, G)
+            if c > 3:
+                chain_out_b(c - 2, G)
+            if c in (1, 2):
+                chain_in_c(c + 3, G)
+                norm_in(c + 4)
+            mx_passes(c, 0, taps, True, whole)
+            if whole:
+                relu(c, 0, S)
+            if c == 0:
+                for k in (6, 7, 8):
+                    w_transpose(k, S)
+                chain_in_c(2, G)
+                norm_in(3)
+            u_mult(c + 1, 0)
+            u_mult(c + 1, 1)
+            if c == 0:
+                for k in (6, 7, 8):
+                    w_quant(k)
+            u_quant(c + 1)
+            u_move(c + 1, 0)
+            u_move(c + 1, 2)
+            for s in scaled.get(c - 1, ()):
+                fin(s)
+            mx_passes(c, 1, taps, True, whole)
+            if whole:
+                relu(c, 1, S)
+            if c > 0:
+                norm_out(c - 1, G)
+            for n in {0: (2,), 1: (3,), 2: (4, 5), 3: (6,), 4: (7,)}.get(c, ()):
+                g_bcast(n)
+            for s in scaled.get(c, ()):
                 t_bcast(s)
-            if 2 * c + 4 < NCH:
-                x_chunk(2 * c + 4)
+            if c == 0:
+                norm_in(4)
+                chain_in_c(3, G)
+            if c == 2:
+                chain_in_c(6, G)
+                norm_in(7)
+
+        for half in range(2):
+            mx_passes(6, half, [2], False, True)
+            relu(6, half, S)
+        chain_out_b(5, G)
+        for half in range(2):
+            mx_passes(7, half, [0, 1, 2], True, True, 0, 256)
+            relu(7, half, V, 0, 256)
+        fin(4)
+        mx_passes(7, 0, [0, 1, 2], True, True, 256, 256)
+        for pg in range(2):
+            r_words(6, pg)
+            r_squares(6, pg)
+        t_bcast(5)
+        r_words(7, 0)
+        r_squares(7, 0)
+        chain_out_a(6, G, 0, 6)
+        mx_passes(7, 1, [0, 1, 2], True, True, 256, 256)
+        relu(7, 0, V, 256, 256)
+        fin(5)
+        relu(7, 1, V, 256, 256)
+        chain_out_b(6, V, 0, 6)
+        r_words(7, 1)
+        r_squares(7, 1)
+        t_bcast(6)
+        fin(6)
+        chain_out_a(7, V, 2, 2)
+        t_bcast(7, 0, 2)
+        finish(7, 0, 0, 2)
+        finish(7, 1, 0, 2)
+        chain_out_b(7, V, 2, 2)
+        t_bcast(7, 2, 2)
+        finish(7, 0, 2, 2)
+        finish(7, 1, 2, 2)

@@ -38,15 +38,16 @@ def tile_pvconv2d_t_kernel(tc, x, Wk, bias, out):
 
         xs = [const.tile([P, 4, H * W], BF16, name="xs%d" % b) for b in range(B)]
         w_sb = const.tile([P, 18, C], BF16, name="w_sb")
-        wk_v = Wk.rearrange("k (h p) c -> p (k h) c", p=P)
-        btile = const.tile([P, P], BF16, name="btile")
+        wk_v = Wk.rearrange("k (p h) c -> p k (h c)", h=2)
+        btile = const.tile([P, O], BF16, name="btile")
 
         def load_x(b, lo, hi):
             xv = x[b].rearrange("(q t) h w -> q t (h w)", t=4)
             nc.sync.dma_start(out=xs[b][:, :, lo * W:hi * W], in_=xv[:, :, lo * W:hi * W])
 
         def load_w(k3):
-            nc.sync.dma_start(out=w_sb[:, 6 * k3:6 * k3 + 6, :], in_=wk_v[:, 6 * k3:6 * k3 + 6, :])
+            nc.sync.dma_start(out=w_sb[:, 6 * k3:6 * k3 + 6, :].rearrange("p (k h) c -> p k (h c)", h=2),
+                              in_=wk_v[:, 3 * k3:3 * k3 + 3, :])
 
         nc.vector.memset(btile[:], 0.0)
         load_x(0, 0, 8)
@@ -55,13 +56,12 @@ def tile_pvconv2d_t_kernel(tc, x, Wk, bias, out):
         load_x(1, 8, 16)
         load_w(0)
         load_w(1)
-        nc.scalar.dma_start(out=btile[0:2, :], in_=bias.rearrange("(h o) -> h o", h=2))
+        nc.scalar.dma_start(out=btile[0:1, :], in_=bias.rearrange("(a n) -> a n", a=1))
+        load_w(2)
         load_x(0, 16, 32)
         load_x(1, 16, 32)
-        load_w(2)
-        for half in range(2):
-            load_x(2, 16 * half, 16 * half + 16)
-            load_x(3, 16 * half, 16 * half + 16)
+        load_x(2, 0, 32)
+        load_x(3, 0, 32)
 
         ident_f = const.tile([P, P], F32, name="ident_f")
         make_identity(nc, ident_f[:])
@@ -87,7 +87,10 @@ def tile_pvconv2d_t_kernel(tc, x, Wk, bias, out):
                 nc.vector.memset(border[:, :, w:w + 1], 0)
 
         names = ["n2", "y4", "z2", "zc", "la", "lb", "rzh", "dd", "gg", "m2", "y2o", "zm", "th", "rzo", "tf"]
-        sm = dict((nm, const.tile([P, 4 * NCH], F32, name="sm_" + nm)) for nm in names)
+        sm = dict((nm, const.tile([P, 4 * NCH + 16], F32, name="sm_" + nm)) for nm in names)
+
+        def out_col(s, k):
+            return 4 * s + k + (10 if s == LAST and k >= 2 else 0)
 
         def cols(nm, lo, n):
             return sm[nm][:, lo:lo + n]
@@ -263,33 +266,41 @@ def tile_pvconv2d_t_kernel(tc, x, Wk, bias, out):
         def r_squares(s, pg):
             for pl in range(2):
                 junk = junkp.tile([P, 2, P], BF16, name="junk2")
-                col = 4 * s + 2 * pg + pl
+                col = out_col(s, 2 * pg + pl)
                 nc.scalar.activation(out=junk[:], in_=r_banks[(s, pg)][:, pl], func=ACT.Square,
                                      accum_out=sm["m2"][:, col:col + 1])
 
         def chain_out_a(s, eng, lo=0, n=4):
-            lo = 4 * s + lo
+            out_pow(s, eng, lo, n)
+            out_z(s, eng, lo, n)
+
+        def out_pow(s, eng, lo=0, n=4):
+            lo = out_col(s, lo)
             eng.tensor_scalar(out=cols("y2o", lo, n), in0=cols("m2", lo, n), scalar1=0.01, scalar2=1e-16,
                               op0=ALU.mult, op1=ALU.max)
             nc.gpsimd.tensor_tensor(out=cols("rzo", lo, n), in0=cols("y2o", lo, n), in1=mhalf8[:, 0:n], op=ALU.pow)
+
+        def out_z(s, eng, lo=0, n=4):
+            lo = out_col(s, lo)
             eng.tensor_tensor(out=cols("zm", lo, n), in0=cols("y2o", lo, n), in1=cols("rzo", lo, n), op=ALU.mult)
 
         def chain_out_b(s, eng, lo=0, n=4):
-            lo = 4 * s + lo
+            lo = out_col(s, lo)
             nc.scalar.activation(out=cols("th", lo, n), in_=cols("zm", lo, n), func=ACT.Tanh)
             eng.tensor_tensor(out=cols("tf", lo, n), in0=cols("th", lo, n), in1=cols("rzo", lo, n), op=ALU.mult)
 
         t_banks = {}
+        out_v = out.rearrange("b (p h) y x -> h b p y x", h=2)
 
         def t_bcast(s, lo=0, n=4):
             if lo == 0:
                 tb_new = bc.tile([P, 4, P], F32, name="tb", tag="bc")
                 t_banks[s] = tb_new
             for k in range(lo, lo + n):
-                nc.tensor.transpose(t_banks[s][:, k, :], sm["tf"][:, 4 * s + k:4 * s + k + 1].to_broadcast([P, P]),
+                nc.tensor.transpose(t_banks[s][:, k, :], sm["tf"][:, out_col(s, k):out_col(s, k) + 1].to_broadcast([P, P]),
                                     ident_f[:])
 
-        def finish(s, half, lo=0, n=4):
+        def finish(s, half, lo=0, n=4, queue=nc.sync):
             bp, hq = divmod(s, 4)
             rows = 2 * n
             tv = t_banks[s][:, lo:lo + n, :].rearrange("p k (a b w) -> p (k a) b w", a=2, b=2)
@@ -297,17 +308,18 @@ def tile_pvconv2d_t_kernel(tc, x, Wk, bias, out):
             rv = r_tiles[(s, half)][:, lo * P:(lo + n) * P].rearrange("p (h b w) -> p h b w", h=rows, b=2)
             nc.vector.tensor_tensor(out=ob[:].rearrange("p b h w -> p h b w"), in0=rv, in1=tv, op=ALU.mult)
             r0 = ROWS * hq + 2 * lo
-            nc.sync.dma_start(
-                out=out[2 * bp:2 * bp + 2, half * P:(half + 1) * P, r0:r0 + rows, :].rearrange("b p h w -> p b (h w)"),
+            queue.dma_start(
+                out=out_v[half][2 * bp:2 * bp + 2, :, r0:r0 + rows, :].rearrange("b p h w -> p b (h w)"),
                 in_=ob[:].rearrange("p b h w -> p b (h w)"),
             )
 
         bias_sb = const.tile([P, 2], F32, name="bias_sb")
 
         def bias_columns():
-            bt = bc.tile([P, P], BF16, name="bt", tag="bc")
-            nc.tensor.transpose(bt[:], btile[:], ident_b[:])
-            nc.vector.tensor_copy(out=bias_sb[:], in_=bt[:, 0:2])
+            bt = bc.tile([P, 2, P], BF16, name="bt", tag="bc")
+            for half in range(2):
+                nc.tensor.transpose(bt[:, half, :], btile[:, half:O:2], ident_b[:])
+            nc.vector.tensor_copy(out=bias_sb[:], in_=bt[:, :, 0:1].rearrange("p h a -> p (h a)"))
 
         def chain_in_ab(c, eng):
             chain_in_a(c, eng)
@@ -342,6 +354,8 @@ def tile_pvconv2d_t_kernel(tc, x, Wk, bias, out):
         u_move(0, 2)
         g_bcast(1)
         bias_columns()
+        for k in (6, 7, 8):
+            w_transpose(k, nc.scalar)
         x_words(2)
         x_squares(2)
         chain_in_ab(2, G)
@@ -366,7 +380,7 @@ def tile_pvconv2d_t_kernel(tc, x, Wk, bias, out):
                 r_squares(s, pg)
             chain_out_a(s, eng)
 
-        scaled = {3: (0,), 4: (1, 2), 5: (3,), 6: (4,)}
+        scaled = {3: (0,), 4: (1,), 5: (2, 3), 6: (4,)}
         for c in range(LAST):
             whole = c % 4 == 3
             taps = [0, 1, 2] if whole else [0, 1]
@@ -387,8 +401,6 @@ def tile_pvconv2d_t_kernel(tc, x, Wk, bias, out):
             if whole:
                 relu(c, 0, S)
             if c == 0:
-                for k in (6, 7, 8):
-                    w_transpose(k, S)
                 chain_in_c(2, G)
                 norm_in(3)
             u_mult(c + 1, 0)
@@ -437,16 +449,18 @@ def tile_pvconv2d_t_kernel(tc, x, Wk, bias, out):
         relu(7, 0, V, 256, 256)
         fin(5)
         relu(7, 1, V, 256, 256)
-        chain_out_b(6, V, 0, 6)
         r_words(7, 1)
         r_squares(7, 1)
+        out_pow(7, V, 2, 2)
+        chain_out_b(6, V, 0, 6)
         t_bcast(6)
-        fin(6)
-        chain_out_a(7, V, 2, 2)
         t_bcast(7, 0, 2)
-        finish(7, 0, 0, 2)
-        finish(7, 1, 0, 2)
+        finish(6, 0)
+        out_z(7, V, 2, 2)
+        finish(6, 1)
         chain_out_b(7, V, 2, 2)
         t_bcast(7, 2, 2)
+        finish(7, 0, 0, 2)
+        finish(7, 1, 0, 2)
         finish(7, 0, 2, 2)
-        finish(7, 1, 2, 2)
+        finish(7, 1, 2, 2, nc.scalar)

@@ -71,6 +71,9 @@ def tile_pvconv2d_t_kernel(tc, x, Wk, bias, out):
         nc.vector.memset(ones1[:], 1.0)
         mhalf8 = const.tile([P, 8], F32, name="mhalf8")
         nc.vector.memset(mhalf8[:], -0.5)
+        tiny = const.tile([P, 2], F32, name="tiny")
+        nc.vector.memset(tiny[:, 0:1], 4e-16)
+        nc.vector.memset(tiny[:, 1:2], 1e-16)
         warm = const.tile([P, 1], F32, name="warm")
         nc.scalar.activation(out=warm[:], in_=ones1[:], func=ACT.Ln)
 
@@ -155,24 +158,31 @@ def tile_pvconv2d_t_kernel(tc, x, Wk, bias, out):
                     nc.scalar.activation(out=junk[:], in_=xv[:, par], func=ACT.Square,
                                          accum_out=sm["n2"][:, col:col + 1])
 
-        def chain_in_a(c, eng):
+        def in_pow(c, eng):
             lo = 4 * c
-            eng.tensor_scalar(out=cols("y4", lo, 4), in0=cols("n2", lo, 4), scalar1=0.04, scalar2=4e-16,
-                              op0=ALU.mult, op1=ALU.max)
+            if eng is nc.vector:
+                nc.vector.tensor_scalar(out=cols("y4", lo, 4), in0=cols("n2", lo, 4), scalar1=0.04, scalar2=4e-16,
+                                        op0=ALU.mult, op1=ALU.max)
+            else:
+                nc.scalar.activation(out=cols("y4", lo, 4), in_=cols("n2", lo, 4), func=ACT.Identity,
+                                     bias=tiny[:, 0:1], scale=0.04)
             nc.gpsimd.tensor_tensor(out=cols("rzh", lo, 4), in0=cols("y4", lo, 4), in1=mhalf8[:, 0:4], op=ALU.pow)
 
-        def chain_in_b(c, eng):
+        def in_z(c):
             lo = 4 * c
-            eng.tensor_tensor(out=cols("z2", lo, 4), in0=cols("y4", lo, 4), in1=cols("rzh", lo, 4), op=ALU.mult)
-            eng.tensor_scalar(out=cols("zc", lo, 4), in0=cols("z2", lo, 4), scalar1=0.5, scalar2=ZMAX,
-                              op0=ALU.mult, op1=ALU.min)
+            nc.vector.tensor_tensor(out=cols("z2", lo, 4), in0=cols("y4", lo, 4), in1=cols("rzh", lo, 4), op=ALU.mult)
+            nc.vector.tensor_scalar(out=cols("zc", lo, 4), in0=cols("z2", lo, 4), scalar1=0.5, scalar2=ZMAX,
+                                    op0=ALU.mult, op1=ALU.min)
 
-        def chain_in_c(c, eng):
+        def in_log(c):
             lo = 4 * c
             nc.scalar.activation(out=cols("la", lo, 4), in_=cols("zc", lo, 4), func=ACT.Ln, bias=ones1[:], scale=1.0)
             nc.scalar.activation(out=cols("lb", lo, 4), in_=cols("zc", lo, 4), func=ACT.Ln, bias=ones1[:], scale=-1.0)
-            eng.tensor_tensor(out=cols("dd", lo, 4), in0=cols("la", lo, 4), in1=cols("lb", lo, 4), op=ALU.subtract)
-            eng.tensor_tensor(out=cols("gg", lo, 4), in0=cols("dd", lo, 4), in1=cols("rzh", lo, 4), op=ALU.mult)
+
+        def in_g(c):
+            lo = 4 * c
+            nc.vector.tensor_tensor(out=cols("dd", lo, 4), in0=cols("la", lo, 4), in1=cols("lb", lo, 4), op=ALU.subtract)
+            nc.vector.tensor_tensor(out=cols("gg", lo, 4), in0=cols("dd", lo, 4), in1=cols("rzh", lo, 4), op=ALU.mult)
 
         g_banks = {}
         u_tiles = {}
@@ -270,24 +280,29 @@ def tile_pvconv2d_t_kernel(tc, x, Wk, bias, out):
                 nc.scalar.activation(out=junk[:], in_=r_banks[(s, pg)][:, pl], func=ACT.Square,
                                      accum_out=sm["m2"][:, col:col + 1])
 
-        def chain_out_a(s, eng, lo=0, n=4):
-            out_pow(s, eng, lo, n)
-            out_z(s, eng, lo, n)
-
-        def out_pow(s, eng, lo=0, n=4):
+        def out_pow(s, lo=0, n=4):
             lo = out_col(s, lo)
-            eng.tensor_scalar(out=cols("y2o", lo, n), in0=cols("m2", lo, n), scalar1=0.01, scalar2=1e-16,
-                              op0=ALU.mult, op1=ALU.max)
+            nc.scalar.activation(out=cols("y2o", lo, n), in_=cols("m2", lo, n), func=ACT.Identity,
+                                 bias=tiny[:, 1:2], scale=0.01)
             nc.gpsimd.tensor_tensor(out=cols("rzo", lo, n), in0=cols("y2o", lo, n), in1=mhalf8[:, 0:n], op=ALU.pow)
 
-        def out_z(s, eng, lo=0, n=4):
+        def out_z(s, lo=0, n=4):
             lo = out_col(s, lo)
-            eng.tensor_tensor(out=cols("zm", lo, n), in0=cols("y2o", lo, n), in1=cols("rzo", lo, n), op=ALU.mult)
+            nc.vector.tensor_tensor(out=cols("zm", lo, n), in0=cols("y2o", lo, n), in1=cols("rzo", lo, n), op=ALU.mult)
 
-        def chain_out_b(s, eng, lo=0, n=4):
+        def out_tanh(s, lo=0, n=4):
             lo = out_col(s, lo)
             nc.scalar.activation(out=cols("th", lo, n), in_=cols("zm", lo, n), func=ACT.Tanh)
-            eng.tensor_tensor(out=cols("tf", lo, n), in0=cols("th", lo, n), in1=cols("rzo", lo, n), op=ALU.mult)
+
+        def out_t(s, lo=0, n=4):
+            lo = out_col(s, lo)
+            nc.vector.tensor_tensor(out=cols("tf", lo, n), in0=cols("th", lo, n), in1=cols("rzo", lo, n), op=ALU.mult)
+
+        def out_scalar(s):
+            for k in range(4):
+                y, rz, th, tf = [sm[nm][:, out_col(s, k):out_col(s, k) + 1] for nm in ("y2o", "rzo", "th", "tf")]
+                nc.scalar.activation(out=th, in_=y, func=ACT.Tanh, scale=rz)
+                nc.scalar.activation(out=tf, in_=th, func=ACT.Copy, scale=rz)
 
         t_banks = {}
         out_v = out.rearrange("b (p h) y x -> h b p y x", h=2)
@@ -321,29 +336,27 @@ def tile_pvconv2d_t_kernel(tc, x, Wk, bias, out):
                 nc.tensor.transpose(bt[:, half, :], btile[:, half:O:2], ident_b[:])
             nc.vector.tensor_copy(out=bias_sb[:], in_=bt[:, :, 0:1].rearrange("p h a -> p (h a)"))
 
-        def chain_in_ab(c, eng):
-            chain_in_a(c, eng)
-            chain_in_b(c, eng)
-
-        V, G = nc.vector, nc.gpsimd
+        V, S = nc.vector, nc.scalar
         clear_borders(0)
         clear_borders(1)
         x_gram(0)
-        chain_in_a(0, V)
+        in_pow(0, V)
         x_gram(1)
-        chain_in_b(0, V)
-        chain_in_c(0, V)
-        chain_in_a(1, V)
+        in_pow(1, V)
+        in_z(0)
+        in_log(0)
+        in_g(0)
         for k in (0, 1, 2):
-            w_transpose(k, nc.scalar)
+            w_transpose(k, S)
         g_bcast(0)
         w_quant(0)
         w_quant(1)
-        chain_in_b(1, V)
-        chain_in_c(1, V)
+        in_z(1)
+        in_log(1)
+        in_g(1)
         w_quant(2)
         for k in (4, 3, 5):
-            w_transpose(k, nc.scalar)
+            w_transpose(k, S)
         u_mult(0, 0)
         u_mult(0, 1)
         w_quant(4)
@@ -355,30 +368,24 @@ def tile_pvconv2d_t_kernel(tc, x, Wk, bias, out):
         g_bcast(1)
         bias_columns()
         for k in (6, 7, 8):
-            w_transpose(k, nc.scalar)
+            w_transpose(k, S)
         x_words(2)
         x_squares(2)
-        chain_in_ab(2, G)
-
-        S = nc.scalar
+        in_pow(2, S)
 
         def fin(s):
             finish(s, 0)
             finish(s, 1)
 
         def norm_in(n):
-            if n in GRAM:
-                x_gram(n)
-            else:
-                x_words(n)
-                x_squares(n)
-            chain_in_ab(n, G)
+            x_words(n)
+            x_squares(n)
+            in_pow(n, S)
 
-        def norm_out(s, eng):
+        def norm_out(s):
             for pg in range(2):
                 r_words(s, pg)
                 r_squares(s, pg)
-            chain_out_a(s, eng)
 
         scaled = {3: (0,), 4: (1,), 5: (2, 3), 6: (4,)}
         for c in range(LAST):
@@ -388,79 +395,97 @@ def tile_pvconv2d_t_kernel(tc, x, Wk, bias, out):
                 for half in range(2):
                     mx_passes(c - 1, half, [2], False, True)
                     relu(c - 1, half, S)
-            if c == 3:
-                chain_in_c(7, G)
-                chain_out_b(0, G)
-                chain_out_b(1, G)
             if c > 3:
-                chain_out_b(c - 2, G)
+                out_scalar(c - 2)
             if c in (1, 2):
-                chain_in_c(c + 3, G)
                 norm_in(c + 4)
             mx_passes(c, 0, taps, True, whole)
             if whole:
                 relu(c, 0, S)
-            if c == 0:
-                chain_in_c(2, G)
-                norm_in(3)
             u_mult(c + 1, 0)
+            if c == 0:
+                in_z(2)
+                norm_in(3)
+                in_log(2)
+            elif c < 4:
+                if c == 3:
+                    in_z(7)
+                    in_log(7)
+                    out_scalar(0)
+                    out_scalar(1)
+                in_g({1: 3, 2: 5, 3: 6}[c])
             u_mult(c + 1, 1)
             if c == 0:
                 for k in (6, 7, 8):
                     w_quant(k)
+            if c == 1:
+                in_z(4)
+                in_log(4)
+            if c == 3:
+                in_g(7)
             u_quant(c + 1)
+            if c == 0:
+                in_g(2)
             u_move(c + 1, 0)
+            if c == 1:
+                in_g(4)
             u_move(c + 1, 2)
             for s in scaled.get(c - 1, ()):
                 fin(s)
+            if c < 3:
+                in_z({0: 3, 1: 5, 2: 6}[c])
             mx_passes(c, 1, taps, True, whole)
             if whole:
                 relu(c, 1, S)
             if c > 0:
-                norm_out(c - 1, G)
+                norm_out(c - 1)
             for n in {0: (2,), 1: (3,), 2: (4, 5), 3: (6,), 4: (7,)}.get(c, ()):
                 g_bcast(n)
             for s in scaled.get(c, ()):
                 t_bcast(s)
+            if c > 0:
+                out_pow(c - 1)
             if c == 0:
                 norm_in(4)
-                chain_in_c(3, G)
+            if c < 3:
+                in_log({0: 3, 1: 5, 2: 6}[c])
             if c == 2:
-                chain_in_c(6, G)
-                norm_in(7)
+                x_gram(7)
+                in_pow(7, V)
 
         for half in range(2):
             mx_passes(6, half, [2], False, True)
             relu(6, half, S)
-        chain_out_b(5, G)
+        out_scalar(5)
         for half in range(2):
             mx_passes(7, half, [0, 1, 2], True, True, 0, 256)
             relu(7, half, V, 0, 256)
         fin(4)
         mx_passes(7, 0, [0, 1, 2], True, True, 256, 256)
-        for pg in range(2):
-            r_words(6, pg)
-            r_squares(6, pg)
+        norm_out(6)
         t_bcast(5)
         r_words(7, 0)
         r_squares(7, 0)
-        chain_out_a(6, G, 0, 6)
+        out_pow(6, 0, 6)
         mx_passes(7, 1, [0, 1, 2], True, True, 256, 256)
         relu(7, 0, V, 256, 256)
         fin(5)
         relu(7, 1, V, 256, 256)
         r_words(7, 1)
         r_squares(7, 1)
-        out_pow(7, V, 2, 2)
-        chain_out_b(6, V, 0, 6)
+        out_pow(7, 2, 2)
+        out_z(6, 0, 6)
+        out_tanh(6, 0, 6)
+        out_t(6, 0, 6)
         t_bcast(6)
         t_bcast(7, 0, 2)
         finish(6, 0)
-        out_z(7, V, 2, 2)
+        out_z(7, 2, 2)
         finish(6, 1)
-        chain_out_b(7, V, 2, 2)
+        out_tanh(7, 2, 2)
+        out_t(7, 2, 2)
         t_bcast(7, 2, 2)
         finish(7, 0, 0, 2)
         finish(7, 1, 0, 2)
         finish(7, 0, 2, 2)
-        finish(7, 1, 2, 2, nc.scalar)
+        finish(7, 1, 2, 2, S)

@@ -19,7 +19,7 @@ ZMAX = 1.0 - 1e-6
 ROWS = 8
 NCH = 8
 PADW = (H + 2) * 64
-GRAM = (0, 1, 7)
+GRAM = (0, 7)
 LAST = NCH - 1
 
 
@@ -36,27 +36,37 @@ def tile_pvconv2d_t_kernel(tc, x, Wk, bias, out):
         bc = ctx.enter_context(tc.psum_pool(name="bc", bufs=3))
         accp = ctx.enter_context(tc.psum_pool(name="accp", bufs=3))
 
-        xs = [const.tile([P, 4, H * W], BF16, name="xs%d" % b) for b in range(B)]
-        w_sb = const.tile([P, 18, C], BF16, name="w_sb")
+        pieces = [(0, 8), (8, 16), (16, 32)]
+        xs = {}
+        for b in range(B):
+            for lo, hi in (pieces if b < 2 else [(0, 32)]):
+                x_tile = const.tile([P, 4, (hi - lo) * W], BF16, name="xs%d_%d" % (b, lo))
+                xs[(b, lo)] = x_tile
+
+        def x_rows(b, hq):
+            lo = min(ROWS * hq, 16) if b < 2 else 0
+            px = (ROWS * hq - lo) * W
+            return xs[(b, lo)][:, :, px:px + ROWS * W]
+
+        w_sb = [const.tile([P, 6, C], BF16, name="w_sb%d" % k3) for k3 in range(3)]
         wk_v = Wk.rearrange("k (p h) c -> p k (h c)", h=2)
-        btile = const.tile([P, O], BF16, name="btile")
+        btile = const.tile([P, 2], BF16, name="btile")
 
         def load_x(b, lo, hi):
             xv = x[b].rearrange("(q t) h w -> q t (h w)", t=4)
-            nc.sync.dma_start(out=xs[b][:, :, lo * W:hi * W], in_=xv[:, :, lo * W:hi * W])
+            nc.sync.dma_start(out=xs[(b, lo)][:], in_=xv[:, :, lo * W:hi * W])
 
         def load_w(k3):
-            nc.sync.dma_start(out=w_sb[:, 6 * k3:6 * k3 + 6, :].rearrange("p (k h) c -> p k (h c)", h=2),
+            nc.sync.dma_start(out=w_sb[k3][:].rearrange("p (k h) c -> p k (h c)", h=2),
                               in_=wk_v[:, 3 * k3:3 * k3 + 3, :])
 
-        nc.vector.memset(btile[:], 0.0)
         load_x(0, 0, 8)
         load_x(1, 0, 8)
         load_x(0, 8, 16)
         load_x(1, 8, 16)
         load_w(0)
         load_w(1)
-        nc.scalar.dma_start(out=btile[0:1, :], in_=bias.rearrange("(a n) -> a n", a=1))
+        nc.scalar.dma_start(out=btile[:], in_=bias.rearrange("(p h) -> p h", h=2))
         load_w(2)
         load_x(0, 16, 32)
         load_x(1, 16, 32)
@@ -65,8 +75,6 @@ def tile_pvconv2d_t_kernel(tc, x, Wk, bias, out):
 
         ident_f = const.tile([P, P], F32, name="ident_f")
         make_identity(nc, ident_f[:])
-        ident_b = const.tile([P, P], BF16, name="ident_b")
-        make_identity(nc, ident_b[:])
         ones1 = const.tile([P, 1], F32, name="ones1")
         nc.vector.memset(ones1[:], 1.0)
         mhalf8 = const.tile([P, 8], F32, name="mhalf8")
@@ -101,14 +109,14 @@ def tile_pvconv2d_t_kernel(tc, x, Wk, bias, out):
         wg = const.tile([P, 18, P, 4], BF16, name="wg", align_bytes=64)
         wc = const.tile([P, 18 * P], U32, name="wc", align_bytes=64)
         ws = const.tile([P, 18 * P], U8, name="ws", align_bytes=64)
-        w_f = w_sb[:].bitcast(F32)
         wg_f = wg[:].bitcast(F32)
 
         def w_transpose(k, eng):
             wt = accp.tile([P, 2, 2, P], F32, name="wt", tag="acc")
             for bl in range(2):
                 for u in range(2):
-                    nc.tensor.transpose(wt[:, bl, u, :], w_f[:, 2 * k + bl, u:2 * P:2], ident_f[:])
+                    w_f = w_sb[k // 3][:].bitcast(F32)
+                    nc.tensor.transpose(wt[:, bl, u, :], w_f[:, 2 * (k % 3) + bl, u:2 * P:2], ident_f[:])
             src = wt[:].rearrange("p b u o -> p b o u")
             if eng is nc.vector:
                 nc.vector.tensor_copy(out=wg_f[:, 2 * k:2 * k + 2, :, :], in_=src)
@@ -124,13 +132,12 @@ def tile_pvconv2d_t_kernel(tc, x, Wk, bias, out):
 
         def x_gram(c):
             bp, hq = divmod(c, 4)
-            pool, tag = (tp, "tp") if c < 2 else (bc, "bc")
+            pool, tag = (tp, "tp") if c == 0 else (bc, "bc")
             gm = pool.tile([P, 4, P], F32, name="gm", tag=tag)
             for k in range(4):
                 b2, q = divmod(k, 2)
-                lo = hq * 256 + q * P
                 for t in range(4):
-                    px = xs[2 * bp + b2][:, t, lo:lo + P]
+                    px = x_rows(2 * bp + b2, hq)[:, t, q * P:q * P + P]
                     nc.tensor.matmul(gm[:, k, :], lhsT=px, rhs=px, start=(t == 0), stop=(t == 3))
             for k in range(4):
                 junk = junkp.tile([P, P], F32, name="junkg")
@@ -143,14 +150,14 @@ def tile_pvconv2d_t_kernel(tc, x, Wk, bias, out):
         def x_words(c):
             bp, hq = divmod(c, 4)
             for b2 in range(2):
-                xf = xs[2 * bp + b2][:].bitcast(F32)
+                xf = x_rows(2 * bp + b2, hq).bitcast(F32)
                 xt = tp.tile([P, 4, P], F32, name="xt", tag="tp")
                 for t in range(4):
-                    nc.tensor.transpose(xt[:, t, :], xf[:, t, hq * P:(hq + 1) * P], ident_f[:])
+                    nc.tensor.transpose(xt[:, t, :], xf[:, t, :], ident_f[:])
                 x_banks[(c, b2)] = xt
 
-        def x_squares(c):
-            for b2 in range(2):
+        def x_squares(c, images=(0, 1)):
+            for b2 in images:
                 xv = x_banks[(c, b2)][:].bitcast(BF16).rearrange("p t (q par) -> p par t q", par=2)
                 for par in range(2):
                     junk = junkp.tile([P, 4, P], BF16, name="junk")
@@ -199,7 +206,7 @@ def tile_pvconv2d_t_kernel(tc, x, Wk, bias, out):
                 uc_new = upool.tile([P, ROWS, 2, W, 4], BF16, name="uc", align_bytes=64)
                 u_tiles[c] = uc_new
             gv = g_banks[c][:, 2 * b2:2 * b2 + 2, :]
-            xv = xs[2 * bp + b2][:, :, hq * 256:(hq + 1) * 256]
+            xv = x_rows(2 * bp + b2, hq)
             uv = u_tiles[c][:, :, b2, :, :]
             if c in GRAM:
                 in0 = xv.rearrange("p t (h w) -> p h w t", w=W)
@@ -265,8 +272,9 @@ def tile_pvconv2d_t_kernel(tc, x, Wk, bias, out):
 
         r_banks = {}
 
-        def r_words(s, pg):
-            rt = tp.tile([P, 2, 2, P], F32, name="rt", tag="tp")
+        def r_words(s, pg, where=(tp, "tp")):
+            pool, tag = where
+            rt = pool.tile([P, 2, 2, P], F32, name="rt", tag=tag)
             for pl in range(2):
                 pb = 2 * pg + pl
                 for half in range(2):
@@ -330,48 +338,44 @@ def tile_pvconv2d_t_kernel(tc, x, Wk, bias, out):
 
         bias_sb = const.tile([P, 2], F32, name="bias_sb")
 
-        def bias_columns():
-            bt = bc.tile([P, 2, P], BF16, name="bt", tag="bc")
-            for half in range(2):
-                nc.tensor.transpose(bt[:, half, :], btile[:, half:O:2], ident_b[:])
-            nc.vector.tensor_copy(out=bias_sb[:], in_=bt[:, :, 0:1].rearrange("p h a -> p (h a)"))
-
         V, S = nc.vector, nc.scalar
         clear_borders(0)
         clear_borders(1)
         x_gram(0)
         in_pow(0, V)
-        x_gram(1)
-        in_pow(1, V)
+        x_words(1)
+        x_squares(1, (0,))
         in_z(0)
         in_log(0)
         in_g(0)
-        for k in (0, 1, 2):
+        x_squares(1, (1,))
+        in_pow(1, S)
+        for k in (1, 0, 2):
             w_transpose(k, S)
         g_bcast(0)
-        w_quant(0)
-        w_quant(1)
-        in_z(1)
-        in_log(1)
-        in_g(1)
-        w_quant(2)
         for k in (4, 3, 5):
             w_transpose(k, S)
         u_mult(0, 0)
+        w_quant(1)
+        in_z(1)
+        in_log(1)
         u_mult(0, 1)
+        in_g(1)
         w_quant(4)
         u_quant(0)
+        w_quant(0)
         w_quant(3)
         u_move(0, 0)
+        w_quant(2)
         w_quant(5)
         u_move(0, 2)
-        g_bcast(1)
-        bias_columns()
+        nc.vector.tensor_copy(out=bias_sb[:], in_=btile[:])
         for k in (6, 7, 8):
             w_transpose(k, S)
         x_words(2)
         x_squares(2)
         in_pow(2, S)
+        g_bcast(1)
 
         def fin(s):
             finish(s, 0)
@@ -391,6 +395,8 @@ def tile_pvconv2d_t_kernel(tc, x, Wk, bias, out):
         for c in range(LAST):
             whole = c % 4 == 3
             taps = [0, 1, 2] if whole else [0, 1]
+            if c == 1:
+                mx_passes(c, 0, taps, True, whole)
             if c % 4 > 0:
                 for half in range(2):
                     mx_passes(c - 1, half, [2], False, True)
@@ -399,14 +405,15 @@ def tile_pvconv2d_t_kernel(tc, x, Wk, bias, out):
                 out_scalar(c - 2)
             if c in (1, 2):
                 norm_in(c + 4)
-            mx_passes(c, 0, taps, True, whole)
+            if c != 1:
+                mx_passes(c, 0, taps, True, whole)
             if whole:
                 relu(c, 0, S)
             u_mult(c + 1, 0)
             if c == 0:
                 in_z(2)
-                norm_in(3)
                 in_log(2)
+                norm_in(3)
             elif c < 4:
                 if c == 3:
                     in_z(7)
@@ -416,20 +423,20 @@ def tile_pvconv2d_t_kernel(tc, x, Wk, bias, out):
                 in_g({1: 3, 2: 5, 3: 6}[c])
             u_mult(c + 1, 1)
             if c == 0:
-                for k in (6, 7, 8):
-                    w_quant(k)
+                in_g(2)
             if c == 1:
                 in_z(4)
                 in_log(4)
             if c == 3:
                 in_g(7)
             u_quant(c + 1)
-            if c == 0:
-                in_g(2)
             u_move(c + 1, 0)
             if c == 1:
                 in_g(4)
             u_move(c + 1, 2)
+            if c == 0:
+                for k in (6, 7, 8):
+                    w_quant(k)
             for s in scaled.get(c - 1, ()):
                 fin(s)
             if c < 3:
@@ -461,31 +468,36 @@ def tile_pvconv2d_t_kernel(tc, x, Wk, bias, out):
             mx_passes(7, half, [0, 1, 2], True, True, 0, 256)
             relu(7, half, V, 0, 256)
         fin(4)
-        mx_passes(7, 0, [0, 1, 2], True, True, 256, 256)
         norm_out(6)
+        out_pow(6)
         t_bcast(5)
-        r_words(7, 0)
+        r_words(7, 0, (accp, "acc"))
         r_squares(7, 0)
-        out_pow(6, 0, 6)
-        mx_passes(7, 1, [0, 1, 2], True, True, 256, 256)
+        out_pow(7, 0, 2)
+        for half in range(2):
+            mx_passes(7, half, [0, 1, 2], True, True, 256, 256)
+        finish(5, 0)
         relu(7, 0, V, 256, 256)
-        fin(5)
+        out_z(6)
+        out_tanh(6)
         relu(7, 1, V, 256, 256)
         r_words(7, 1)
         r_squares(7, 1)
         out_pow(7, 2, 2)
-        out_z(6, 0, 6)
-        out_tanh(6, 0, 6)
-        out_t(6, 0, 6)
+        out_t(6)
         t_bcast(6)
-        t_bcast(7, 0, 2)
+        finish(5, 1)
+        out_z(7, 0, 2)
+        out_tanh(7, 0, 2)
         finish(6, 0)
-        out_z(7, 2, 2)
+        out_t(7, 0, 2)
+        t_bcast(7, 0, 2)
         finish(6, 1)
+        out_z(7, 2, 2)
         out_tanh(7, 2, 2)
+        finish(7, 0, 0, 2)
         out_t(7, 2, 2)
         t_bcast(7, 2, 2)
-        finish(7, 0, 0, 2)
         finish(7, 1, 0, 2)
         finish(7, 0, 2, 2)
         finish(7, 1, 2, 2, S)

@@ -175,9 +175,12 @@ def tile_pvconv2d_t_kernel(tc, x, Wk, bias, out):
                                      bias=tiny[:, 0:1], scale=0.04)
             nc.gpsimd.tensor_tensor(out=cols("rzh", lo, 4), in0=cols("y4", lo, 4), in1=mhalf8[:, 0:4], op=ALU.pow)
 
-        def in_z(c):
+        def in_z2(c):
             lo = 4 * c
             nc.vector.tensor_tensor(out=cols("z2", lo, 4), in0=cols("y4", lo, 4), in1=cols("rzh", lo, 4), op=ALU.mult)
+
+        def in_zc(c):
+            lo = 4 * c
             nc.vector.tensor_scalar(out=cols("zc", lo, 4), in0=cols("z2", lo, 4), scalar1=0.5, scalar2=ZMAX,
                                     op0=ALU.mult, op1=ALU.min)
 
@@ -186,9 +189,12 @@ def tile_pvconv2d_t_kernel(tc, x, Wk, bias, out):
             nc.scalar.activation(out=cols("la", lo, 4), in_=cols("zc", lo, 4), func=ACT.Ln, bias=ones1[:], scale=1.0)
             nc.scalar.activation(out=cols("lb", lo, 4), in_=cols("zc", lo, 4), func=ACT.Ln, bias=ones1[:], scale=-1.0)
 
-        def in_g(c):
+        def in_dd(c):
             lo = 4 * c
             nc.vector.tensor_tensor(out=cols("dd", lo, 4), in0=cols("la", lo, 4), in1=cols("lb", lo, 4), op=ALU.subtract)
+
+        def in_gg(c):
+            lo = 4 * c
             nc.vector.tensor_tensor(out=cols("gg", lo, 4), in0=cols("dd", lo, 4), in1=cols("rzh", lo, 4), op=ALU.mult)
 
         g_banks = {}
@@ -225,7 +231,7 @@ def tile_pvconv2d_t_kernel(tc, x, Wk, bias, out):
                                   scales=planes[1][bp][:, lo:lo + 512],
                                   in_=u_tiles[c][:].rearrange("p h b w t -> p (h b w t)"))
 
-        def u_move(c, j):
+        def u_move(c, j, scales):
             bp, hq = divmod(c, 4)
             lo = (ROWS * hq + 1) * 64
 
@@ -233,9 +239,11 @@ def tile_pvconv2d_t_kernel(tc, x, Wk, bias, out):
                 return t[:, lo:lo + 512].rearrange("p (r w) -> p r w", w=W)
 
             dst, src = (slice(1, W), slice(0, W - 1)) if j == 0 else (slice(0, W - 1), slice(1, W))
-            nc.vector.tensor_copy(out=rows_of(codes[j][bp][:].bitcast(I32))[:, :, dst],
-                                  in_=rows_of(codes[1][bp][:].bitcast(I32))[:, :, src])
-            nc.vector.tensor_copy(out=rows_of(planes[j][bp])[:, :, dst], in_=rows_of(planes[1][bp])[:, :, src])
+            if scales:
+                nc.vector.tensor_copy(out=rows_of(planes[j][bp])[:, :, dst], in_=rows_of(planes[1][bp])[:, :, src])
+            else:
+                nc.vector.tensor_copy(out=rows_of(codes[j][bp][:].bitcast(I32))[:, :, dst],
+                                      in_=rows_of(codes[1][bp][:].bitcast(I32))[:, :, src])
 
         accs = {}
         r_tiles = {}
@@ -306,27 +314,26 @@ def tile_pvconv2d_t_kernel(tc, x, Wk, bias, out):
             lo = out_col(s, lo)
             nc.vector.tensor_tensor(out=cols("tf", lo, n), in0=cols("th", lo, n), in1=cols("rzo", lo, n), op=ALU.mult)
 
-        def out_scalar(s):
-            for k in range(4):
-                y, rz, th, tf = [sm[nm][:, out_col(s, k):out_col(s, k) + 1] for nm in ("y2o", "rzo", "th", "tf")]
-                nc.scalar.activation(out=th, in_=y, func=ACT.Tanh, scale=rz)
-                nc.scalar.activation(out=tf, in_=th, func=ACT.Copy, scale=rz)
+        def out_scalar(s, lo=0, n=4):
+            for dst, func, src in (("th", ACT.Tanh, "y2o"), ("tf", ACT.Copy, "th")):
+                for k in range(lo, lo + n):
+                    at = slice(out_col(s, k), out_col(s, k) + 1)
+                    nc.scalar.activation(out=sm[dst][:, at], in_=sm[src][:, at], func=func, scale=sm["rzo"][:, at])
 
         t_banks = {}
         out_v = out.rearrange("b (p h) y x -> h b p y x", h=2)
 
         def t_bcast(s, lo=0, n=4):
-            if lo == 0:
-                tb_new = bc.tile([P, 4, P], F32, name="tb", tag="bc")
-                t_banks[s] = tb_new
-            for k in range(lo, lo + n):
-                nc.tensor.transpose(t_banks[s][:, k, :], sm["tf"][:, out_col(s, k):out_col(s, k) + 1].to_broadcast([P, P]),
-                                    ident_f[:])
+            tb = bc.tile([P, 4, P], F32, name="tb", tag="bc")
+            t_banks[(s, lo)] = tb
+            for k in range(n):
+                col = out_col(s, lo + k)
+                nc.tensor.transpose(tb[:, k, :], sm["tf"][:, col:col + 1].to_broadcast([P, P]), ident_f[:])
 
         def finish(s, half, lo=0, n=4, queue=nc.sync):
             bp, hq = divmod(s, 4)
             rows = 2 * n
-            tv = t_banks[s][:, lo:lo + n, :].rearrange("p k (a b w) -> p (k a) b w", a=2, b=2)
+            tv = t_banks[(s, lo)][:, 0:n, :].rearrange("p k (a b w) -> p (k a) b w", a=2, b=2)
             ob = opool.tile([P, 2, rows, W], F32, name="ob%d" % rows)
             rv = r_tiles[(s, half)][:, lo * P:(lo + n) * P].rearrange("p (h b w) -> p h b w", h=rows, b=2)
             nc.vector.tensor_tensor(out=ob[:].rearrange("p b h w -> p h b w"), in0=rv, in1=tv, op=ALU.mult)
@@ -345,9 +352,11 @@ def tile_pvconv2d_t_kernel(tc, x, Wk, bias, out):
         in_pow(0, V)
         x_words(1)
         x_squares(1, (0,))
-        in_z(0)
+        in_z2(0)
+        in_zc(0)
         in_log(0)
-        in_g(0)
+        in_dd(0)
+        in_gg(0)
         x_squares(1, (1,))
         in_pow(1, S)
         for k in (1, 0, 2):
@@ -357,18 +366,22 @@ def tile_pvconv2d_t_kernel(tc, x, Wk, bias, out):
             w_transpose(k, S)
         u_mult(0, 0)
         w_quant(1)
-        in_z(1)
-        in_log(1)
+        in_z2(1)
         u_mult(0, 1)
-        in_g(1)
+        in_zc(1)
         w_quant(4)
         u_quant(0)
+        in_log(1)
+        in_dd(1)
         w_quant(0)
+        in_gg(1)
+        u_move(0, 0, False)
         w_quant(3)
-        u_move(0, 0)
+        u_move(0, 0, True)
+        u_move(0, 2, False)
         w_quant(2)
+        u_move(0, 2, True)
         w_quant(5)
-        u_move(0, 2)
         nc.vector.tensor_copy(out=bias_sb[:], in_=btile[:])
         for k in (6, 7, 8):
             w_transpose(k, S)
@@ -409,38 +422,60 @@ def tile_pvconv2d_t_kernel(tc, x, Wk, bias, out):
                 mx_passes(c, 0, taps, True, whole)
             if whole:
                 relu(c, 0, S)
+            fins = [(s, half) for s in scaled.get(c - 1, ()) for half in range(2)]
             u_mult(c + 1, 0)
             if c == 0:
-                in_z(2)
+                w_quant(6)
+                in_z2(2)
+                w_quant(7)
+                in_zc(2)
                 in_log(2)
                 norm_in(3)
-            elif c < 4:
-                if c == 3:
-                    in_z(7)
-                    in_log(7)
-                    out_scalar(0)
-                    out_scalar(1)
-                in_g({1: 3, 2: 5, 3: 6}[c])
-            u_mult(c + 1, 1)
-            if c == 0:
-                in_g(2)
+                w_quant(8)
+                in_dd(2)
+                in_gg(2)
             if c == 1:
-                in_z(4)
-                in_log(4)
+                in_dd(3)
+            if c == 2:
+                in_dd(4)
+                in_z2(5)
             if c == 3:
-                in_g(7)
-            u_quant(c + 1)
-            u_move(c + 1, 0)
+                in_dd(6)
+                in_z2(7)
+            u_mult(c + 1, 1)
             if c == 1:
-                in_g(4)
-            u_move(c + 1, 2)
+                in_gg(3)
+                in_z2(4)
+            if c == 2:
+                in_gg(4)
+                in_zc(5)
+                in_log(5)
+            if c == 3:
+                in_gg(6)
+                in_zc(7)
+                in_log(7)
+                out_scalar(0)
+                out_scalar(1)
+            u_quant(c + 1)
+            if c == 1:
+                in_zc(4)
+                in_log(4)
+            u_move(c + 1, 0, False)
+            if c in (2, 3):
+                in_dd({2: 5, 3: 7}[c])
+            u_move(c + 1, 0, True)
+            if c in (2, 3):
+                in_gg({2: 5, 3: 7}[c])
+            u_move(c + 1, 2, False)
             if c == 0:
-                for k in (6, 7, 8):
-                    w_quant(k)
-            for s in scaled.get(c - 1, ()):
-                fin(s)
-            if c < 3:
-                in_z({0: 3, 1: 5, 2: 6}[c])
+                in_z2(3)
+            u_move(c + 1, 2, True)
+            if c == 0:
+                in_zc(3)
+            if c == 2:
+                in_z2(6)
+            for s, half in fins:
+                finish(s, half)
             mx_passes(c, 1, taps, True, whole)
             if whole:
                 relu(c, 1, S)
@@ -454,11 +489,12 @@ def tile_pvconv2d_t_kernel(tc, x, Wk, bias, out):
                 out_pow(c - 1)
             if c == 0:
                 norm_in(4)
-            if c < 3:
-                in_log({0: 3, 1: 5, 2: 6}[c])
             if c == 2:
                 x_gram(7)
                 in_pow(7, V)
+                in_zc(6)
+            if c in (0, 2):
+                in_log({0: 3, 2: 6}[c])
 
         for half in range(2):
             mx_passes(6, half, [2], False, True)
@@ -480,24 +516,20 @@ def tile_pvconv2d_t_kernel(tc, x, Wk, bias, out):
         relu(7, 0, V, 256, 256)
         out_z(6)
         out_tanh(6)
-        relu(7, 1, V, 256, 256)
+        relu(7, 1, S, 256, 256)
+        out_t(6)
+        out_scalar(7, 0, 2)
         r_words(7, 1)
         r_squares(7, 1)
         out_pow(7, 2, 2)
-        out_t(6)
         t_bcast(6)
-        finish(5, 1)
-        out_z(7, 0, 2)
-        out_tanh(7, 0, 2)
-        finish(6, 0)
-        out_t(7, 0, 2)
         t_bcast(7, 0, 2)
+        finish(5, 1)
+        finish(6, 0)
         finish(6, 1)
-        out_z(7, 2, 2)
-        out_tanh(7, 2, 2)
-        finish(7, 0, 0, 2)
-        out_t(7, 2, 2)
+        out_scalar(7, 2, 2)
         t_bcast(7, 2, 2)
+        finish(7, 0, 0, 2)
         finish(7, 1, 0, 2)
         finish(7, 0, 2, 2)
         finish(7, 1, 2, 2, S)

@@ -60,6 +60,8 @@ def tile_pvconv2d_t_kernel(tc, x, Wk, bias, out):
             nc.sync.dma_start(out=w_sb[k3][:].rearrange("p (k h) c -> p k (h c)", h=2),
                               in_=wk_v[:, 3 * k3:3 * k3 + 3, :])
 
+        zeros = const.tile([P, 512], BF16, name="zeros")
+        nc.vector.memset(zeros[:], 0.0)
         load_x(0, 0, 8)
         load_x(1, 0, 8)
         load_x(0, 8, 16)
@@ -67,9 +69,9 @@ def tile_pvconv2d_t_kernel(tc, x, Wk, bias, out):
         load_w(0)
         load_w(1)
         nc.scalar.dma_start(out=btile[:], in_=bias.rearrange("(p h) -> p h", h=2))
-        load_w(2)
         load_x(0, 16, 32)
         load_x(1, 16, 32)
+        load_w(2)
         load_x(2, 0, 32)
         load_x(3, 0, 32)
 
@@ -130,10 +132,12 @@ def tile_pvconv2d_t_kernel(tc, x, Wk, bias, out):
                 in_=wg[:, 2 * k:2 * k + 2, :, :].rearrange("p b o t -> p (b o t)"),
             )
 
-        def x_gram(c):
+        def x_gram(c, warm_ups=0):
             bp, hq = divmod(c, 4)
             pool, tag = (tp, "tp") if c == 0 else (bc, "bc")
             gm = pool.tile([P, 4, P], F32, name="gm", tag=tag)
+            for m in range(warm_ups):
+                nc.tensor.matmul(gm[:].rearrange("p k n -> p (k n)"), lhsT=zeros[:, 0:P], rhs=zeros[:], start=True, stop=True)
             for k in range(4):
                 b2, q = divmod(k, 2)
                 for t in range(4):
@@ -348,7 +352,7 @@ def tile_pvconv2d_t_kernel(tc, x, Wk, bias, out):
         V, S = nc.vector, nc.scalar
         clear_borders(0)
         clear_borders(1)
-        x_gram(0)
+        x_gram(0, 3)
         in_pow(0, V)
         x_words(1)
         x_squares(1, (0,))
@@ -362,19 +366,20 @@ def tile_pvconv2d_t_kernel(tc, x, Wk, bias, out):
         for k in (1, 0, 2):
             w_transpose(k, S)
         g_bcast(0)
-        for k in (4, 3, 5):
+        for k in (4, 3):
             w_transpose(k, S)
         u_mult(0, 0)
-        w_quant(1)
         in_z2(1)
-        u_mult(0, 1)
+        w_quant(1)
         in_zc(1)
-        w_quant(4)
-        u_quant(0)
         in_log(1)
+        w_transpose(5, S)
+        u_mult(0, 1)
         in_dd(1)
-        w_quant(0)
+        w_quant(4)
         in_gg(1)
+        u_quant(0)
+        w_quant(0)
         u_move(0, 0, False)
         w_quant(3)
         u_move(0, 0, True)
@@ -383,8 +388,6 @@ def tile_pvconv2d_t_kernel(tc, x, Wk, bias, out):
         u_move(0, 2, True)
         w_quant(5)
         nc.vector.tensor_copy(out=bias_sb[:], in_=btile[:])
-        for k in (6, 7, 8):
-            w_transpose(k, S)
         x_words(2)
         x_squares(2)
         in_pow(2, S)
@@ -423,17 +426,15 @@ def tile_pvconv2d_t_kernel(tc, x, Wk, bias, out):
             if whole:
                 relu(c, 0, S)
             fins = [(s, half) for s in scaled.get(c - 1, ()) for half in range(2)]
+            if c == 0:
+                for k in (6, 7, 8):
+                    w_transpose(k, S)
             u_mult(c + 1, 0)
             if c == 0:
-                w_quant(6)
                 in_z2(2)
-                w_quant(7)
                 in_zc(2)
                 in_log(2)
                 norm_in(3)
-                w_quant(8)
-                in_dd(2)
-                in_gg(2)
             if c == 1:
                 in_dd(3)
             if c == 2:
@@ -443,6 +444,8 @@ def tile_pvconv2d_t_kernel(tc, x, Wk, bias, out):
                 in_dd(6)
                 in_z2(7)
             u_mult(c + 1, 1)
+            if c == 0:
+                in_dd(2)
             if c == 1:
                 in_gg(3)
                 in_z2(4)
@@ -457,6 +460,8 @@ def tile_pvconv2d_t_kernel(tc, x, Wk, bias, out):
                 out_scalar(0)
                 out_scalar(1)
             u_quant(c + 1)
+            if c == 0:
+                in_gg(2)
             if c == 1:
                 in_zc(4)
                 in_log(4)
@@ -467,11 +472,13 @@ def tile_pvconv2d_t_kernel(tc, x, Wk, bias, out):
             if c in (2, 3):
                 in_gg({2: 5, 3: 7}[c])
             u_move(c + 1, 2, False)
-            if c == 0:
-                in_z2(3)
             u_move(c + 1, 2, True)
             if c == 0:
+                w_quant(6)
+                in_z2(3)
+                w_quant(7)
                 in_zc(3)
+                w_quant(8)
             if c == 2:
                 in_z2(6)
             for s, half in fins:

@@ -114,7 +114,8 @@ def tile_pvconv2d_t_kernel(tc, x, Wk, bias, out):
         wg_f = wg[:].bitcast(F32)
 
         def w_transpose(k, eng):
-            wt = accp.tile([P, 2, 2, P], F32, name="wt", tag="acc")
+            pool, tag = (bc, "bc") if k in (6, 7) else (accp, "acc")
+            wt = pool.tile([P, 2, 2, P], F32, name="wt", tag=tag)
             for bl in range(2):
                 for u in range(2):
                     w_f = w_sb[k // 3][:].bitcast(F32)
@@ -151,11 +152,12 @@ def tile_pvconv2d_t_kernel(tc, x, Wk, bias, out):
 
         x_banks = {}
 
-        def x_words(c):
+        def x_words(c, where=(tp, "tp")):
             bp, hq = divmod(c, 4)
+            pool, tag = where
             for b2 in range(2):
                 xf = x_rows(2 * bp + b2, hq).bitcast(F32)
-                xt = tp.tile([P, 4, P], F32, name="xt", tag="tp")
+                xt = pool.tile([P, 4, P], F32, name="xt", tag=tag)
                 for t in range(4):
                     nc.tensor.transpose(xt[:, t, :], xf[:, t, :], ident_f[:])
                 x_banks[(c, b2)] = xt
@@ -419,8 +421,11 @@ def tile_pvconv2d_t_kernel(tc, x, Wk, bias, out):
                     relu(c - 1, half, S)
             if c > 3:
                 out_scalar(c - 2)
-            if c in (1, 2):
-                norm_in(c + 4)
+            if c == 1:
+                norm_in(5)
+            if c == 2:
+                x_squares(6)
+                in_pow(6, S)
             if c != 1:
                 mx_passes(c, 0, taps, True, whole)
             if whole:
@@ -494,8 +499,11 @@ def tile_pvconv2d_t_kernel(tc, x, Wk, bias, out):
                 t_bcast(s)
             if c > 0:
                 out_pow(c - 1)
+            if c < 2:
+                x_words((4, 6)[c], (bc, "bc"))
             if c == 0:
-                norm_in(4)
+                x_squares(4)
+                in_pow(4, S)
             if c == 2:
                 x_gram(7)
                 in_pow(7, V)

from contextlib import ExitStack

import concourse.mybir as mybir
from concourse.masks import make_identity

FP8X4 = mybir.dt.float8_e4m3fn_x4
BF16 = mybir.dt.bfloat16
F32 = mybir.dt.float32
I32 = mybir.dt.int32
U32 = mybir.dt.uint32
U8 = mybir.dt.uint8
ALU = mybir.AluOpType
ACT = mybir.ActivationFunctionType

P = 128
B, C, O, H, W = 4, 512, 256, 32, 32
FLOPS = 2 * B * H * W * C * 9 * O
ZMAX = 1.0 - 1e-6
ROWS = 8
NCH = 8
PADW = (H + 2) * 64
GRAM = (0, 7)
LAST = NCH - 1


def tile_pvconv2d_t_kernel(tc, x, Wk, bias, out):
    nc = tc.nc
    with ExitStack() as ctx:
        ctx.enter_context(tc.manual_schedule())
        const = ctx.enter_context(tc.tile_pool(name="const", bufs=1))
        upool = ctx.enter_context(tc.tile_pool(name="upool", bufs=2))
        junkp = ctx.enter_context(tc.tile_pool(name="junkp", bufs=2))
        rpool = ctx.enter_context(tc.tile_pool(name="rpool", bufs=12))
        opool = ctx.enter_context(tc.tile_pool(name="opool", bufs=6))
        tp = ctx.enter_context(tc.psum_pool(name="tp", bufs=2))
        bc = ctx.enter_context(tc.psum_pool(name="bc", bufs=3))
        accp = ctx.enter_context(tc.psum_pool(name="accp", bufs=3))

        pieces = [(0, 8), (8, 16), (16, 32)]
        xs = {}
        for b in range(B):
            for lo, hi in (pieces if b < 2 else [(0, 32)]):
                x_tile = const.tile([P, 4, (hi - lo) * W], BF16, name="xs%d_%d" % (b, lo))
                xs[(b, lo)] = x_tile

        def x_rows(b, hq):
            lo = min(ROWS * hq, 16) if b < 2 else 0
            px = (ROWS * hq - lo) * W
            return xs[(b, lo)][:, :, px:px + ROWS * W]

        w_sb = [const.tile([P, 6, C], BF16, name="w_sb%d" % k3) for k3 in range(3)]
        wk_v = Wk.rearrange("k (p h) c -> p k (h c)", h=2)
        btile = const.tile([P, 2], BF16, name="btile")

        def load_x(b, lo, hi):
            xv = x[b].rearrange("(q t) h w -> q t (h w)", t=4)
            nc.sync.dma_start(out=xs[(b, lo)][:], in_=xv[:, :, lo * W:hi * W])

        def load_w(k3):
            nc.sync.dma_start(out=w_sb[k3][:].rearrange("p (k h) c -> p k (h c)", h=2),
                              in_=wk_v[:, 3 * k3:3 * k3 + 3, :])

        zeros = const.tile([P, 512], BF16, name="zeros")
        nc.vector.memset(zeros[:], 0.0)
        load_x(0, 0, 8)
        load_x(1, 0, 8)
        load_x(0, 8, 16)
        load_x(1, 8, 16)
        load_w(0)
        load_w(1)
        nc.scalar.dma_start(out=btile[:], in_=bias.rearrange("(p h) -> p h", h=2))
        load_x(0, 16, 32)
        load_x(1, 16, 32)
        load_w(2)
        load_x(2, 0, 32)
        load_x(3, 0, 32)

        ident_f = const.tile([P, P], F32, name="ident_f")
        make_identity(nc, ident_f[:])
        ones1 = const.tile([P, 1], F32, name="ones1")
        nc.vector.memset(ones1[:], 1.0)
        mhalf8 = const.tile([P, 8], F32, name="mhalf8")
        nc.vector.memset(mhalf8[:], -0.5)
        tiny = const.tile([P, 2], F32, name="tiny")
        nc.vector.memset(tiny[:, 0:1], 4e-16)
        nc.vector.memset(tiny[:, 1:2], 1e-16)
        warm = const.tile([P, 1], F32, name="warm")
        nc.scalar.activation(out=warm[:], in_=ones1[:], func=ACT.Ln)

        codes = [[const.tile([P, PADW], U32, name="codes%d%d" % (j, bp), align_bytes=64) for bp in range(2)] for j in range(3)]
        planes = [[const.tile([P, PADW], U8, name="planes%d%d" % (j, bp), align_bytes=64) for bp in range(2)] for j in range(3)]

        def clear_borders(bp):
            for j in range(3):
                nc.gpsimd.memset(planes[j][bp][:].bitcast(I32), 0)
                for lo in (0, PADW - 64):
                    nc.vector.memset(codes[j][bp][:, lo:lo + 64].bitcast(I32), 0)
            for j, w in ((0, 0), (2, W - 1)):
                border = codes[j][bp][:].bitcast(I32).rearrange("p (r w) -> p r w", w=W)
                nc.vector.memset(border[:, :, w:w + 1], 0)

        names = ["n2", "y4", "z2", "zc", "la", "lb", "rzh", "dd", "gg", "m2", "y2o", "zm", "th", "rzo", "tf"]
        sm = dict((nm, const.tile([P, 4 * NCH + 16], F32, name="sm_" + nm)) for nm in names)

        def out_col(s, k):
            return 4 * s + k + (10 if s == LAST and k >= 2 else 0)

        def cols(nm, lo, n):
            return sm[nm][:, lo:lo + n]

        wg = const.tile([P, 18, P, 4], BF16, name="wg", align_bytes=64)
        wc = const.tile([P, 18 * P], U32, name="wc", align_bytes=64)
        ws = const.tile([P, 18 * P], U8, name="ws", align_bytes=64)
        wg_f = wg[:].bitcast(F32)

        def w_transpose(k, eng):
            pool, tag = (bc, "bc") if k in (6, 7) else (accp, "acc")
            wt = pool.tile([P, 2, 2, P], F32, name="wt", tag=tag)
            for bl in range(2):
                for u in range(2):
                    w_f = w_sb[k // 3][:].bitcast(F32)
                    nc.tensor.transpose(wt[:, bl, u, :], w_f[:, 2 * (k % 3) + bl, u:2 * P:2], ident_f[:])
            src = wt[:].rearrange("p b u o -> p b o u")
            if eng is nc.vector:
                nc.vector.tensor_copy(out=wg_f[:, 2 * k:2 * k + 2, :, :], in_=src)
            else:
                nc.scalar.copy(out=wg_f[:, 2 * k:2 * k + 2, :, :], in_=src)

        def w_quant(k):
            nc.vector.quantize_mx(
                out=wc[:, 256 * k:256 * k + 256].bitcast(FP8X4),
                scales=ws[:, 256 * k:256 * k + 256],
                in_=wg[:, 2 * k:2 * k + 2, :, :].rearrange("p b o t -> p (b o t)"),
            )

        def x_gram(c, warm_ups=0):
            bp, hq = divmod(c, 4)
            pool, tag = (tp, "tp") if c == 0 else (bc, "bc")
            gm = pool.tile([P, 4, P], F32, name="gm", tag=tag)
            for m in range(warm_ups):
                nc.tensor.matmul(gm[:].rearrange("p k n -> p (k n)"), lhsT=zeros[:, 0:P], rhs=zeros[:], start=True, stop=True)
            for k in range(4):
                b2, q = divmod(k, 2)
                for t in range(4):
                    px = x_rows(2 * bp + b2, hq)[:, t, q * P:q * P + P]
                    nc.tensor.matmul(gm[:, k, :], lhsT=px, rhs=px, start=(t == 0), stop=(t == 3))
            for k in range(4):
                junk = junkp.tile([P, P], F32, name="junkg")
                nc.vector.scalar_tensor_tensor(out=junk[:], in0=gm[:, k, :], scalar=1.0, in1=ident_f[:],
                                               op0=ALU.mult, op1=ALU.mult,
                                               accum_out=sm["n2"][:, 4 * c + k:4 * c + k + 1])

        x_banks = {}

        def x_words(c, where=(tp, "tp")):
            bp, hq = divmod(c, 4)
            pool, tag = where
            for b2 in range(2):
                xf = x_rows(2 * bp + b2, hq).bitcast(F32)
                xt = pool.tile([P, 4, P], F32, name="xt", tag=tag)
                for t in range(4):
                    nc.tensor.transpose(xt[:, t, :], xf[:, t, :], ident_f[:])
                x_banks[(c, b2)] = xt

        def x_squares(c, images=(0, 1)):
            for b2 in images:
                xv = x_banks[(c, b2)][:].bitcast(BF16).rearrange("p t (q par) -> p par t q", par=2)
                for par in range(2):
                    junk = junkp.tile([P, 4, P], BF16, name="junk")
                    col = 4 * c + 2 * b2 + par
                    nc.scalar.activation(out=junk[:], in_=xv[:, par], func=ACT.Square,
                                         accum_out=sm["n2"][:, col:col + 1])

        def in_pow(c, eng):
            lo = 4 * c
            if eng is nc.vector:
                nc.vector.tensor_scalar(out=cols("y4", lo, 4), in0=cols("n2", lo, 4), scalar1=0.04, scalar2=4e-16,
                                        op0=ALU.mult, op1=ALU.max)
            else:
                nc.scalar.activation(out=cols("y4", lo, 4), in_=cols("n2", lo, 4), func=ACT.Identity,
                                     bias=tiny[:, 0:1], scale=0.04)
            nc.gpsimd.tensor_tensor(out=cols("rzh", lo, 4), in0=cols("y4", lo, 4), in1=mhalf8[:, 0:4], op=ALU.pow)

        def in_z2(c):
            lo = 4 * c
            nc.vector.tensor_tensor(out=cols("z2", lo, 4), in0=cols("y4", lo, 4), in1=cols("rzh", lo, 4), op=ALU.mult)

        def in_zc(c):
            lo = 4 * c
            nc.vector.tensor_scalar(out=cols("zc", lo, 4), in0=cols("z2", lo, 4), scalar1=0.5, scalar2=ZMAX,
                                    op0=ALU.mult, op1=ALU.min)

        def in_log(c):
            lo = 4 * c
            nc.scalar.activation(out=cols("la", lo, 4), in_=cols("zc", lo, 4), func=ACT.Ln, bias=ones1[:], scale=1.0)
            nc.scalar.activation(out=cols("lb", lo, 4), in_=cols("zc", lo, 4), func=ACT.Ln, bias=ones1[:], scale=-1.0)

        def in_dd(c):
            lo = 4 * c
            nc.vector.tensor_tensor(out=cols("dd", lo, 4), in0=cols("la", lo, 4), in1=cols("lb", lo, 4), op=ALU.subtract)

        def in_gg(c):
            lo = 4 * c
            nc.vector.tensor_tensor(out=cols("gg", lo, 4), in0=cols("dd", lo, 4), in1=cols("rzh", lo, 4), op=ALU.mult)

        g_banks = {}
        u_tiles = {}

        def g_bcast(c):
            gb = bc.tile([P, 4, P], F32, name="gb", tag="bc")
            for k in range(4):
                nc.tensor.transpose(gb[:, k, :], sm["gg"][:, 4 * c + k:4 * c + k + 1].to_broadcast([P, P]), ident_f[:])
            g_banks[c] = gb

        def u_mult(c, b2):
            bp, hq = divmod(c, 4)
            if b2 == 0:
                uc_new = upool.tile([P, ROWS, 2, W, 4], BF16, name="uc", align_bytes=64)
                u_tiles[c] = uc_new
            gv = g_banks[c][:, 2 * b2:2 * b2 + 2, :]
            xv = x_rows(2 * bp + b2, hq)
            uv = u_tiles[c][:, :, b2, :, :]
            if c in GRAM:
                in0 = xv.rearrange("p t (h w) -> p h w t", w=W)
                in1 = gv.rearrange("p q (h w) -> p (q h) w", w=W).unsqueeze(3).to_broadcast([P, ROWS, W, 4])
                nc.vector.tensor_tensor(out=uv, in0=in0, in1=in1, op=ALU.mult)
            else:
                in0 = xv.rearrange("p t (h w2 par) -> p h w2 par t", h=ROWS, par=2)
                in1 = gv.rearrange("p par (h w2) -> p h w2 par", h=ROWS).unsqueeze(4).to_broadcast([P, ROWS, 16, 2, 4])
                nc.vector.tensor_tensor(out=uv.rearrange("p h (w2 par) t -> p h w2 par t", par=2), in0=in0, in1=in1,
                                        op=ALU.mult)

        def u_quant(c):
            bp, hq = divmod(c, 4)
            lo = (ROWS * hq + 1) * 64
            nc.vector.quantize_mx(out=codes[1][bp][:, lo:lo + 512].bitcast(FP8X4),
                                  scales=planes[1][bp][:, lo:lo + 512],
                                  in_=u_tiles[c][:].rearrange("p h b w t -> p (h b w t)"))

        def u_move(c, j, scales):
            bp, hq = divmod(c, 4)
            lo = (ROWS * hq + 1) * 64

            def rows_of(t):
                return t[:, lo:lo + 512].rearrange("p (r w) -> p r w", w=W)

            dst, src = (slice(1, W), slice(0, W - 1)) if j == 0 else (slice(0, W - 1), slice(1, W))
            if scales:
                nc.vector.tensor_copy(out=rows_of(planes[j][bp])[:, :, dst], in_=rows_of(planes[1][bp])[:, :, src])
            else:
                nc.vector.tensor_copy(out=rows_of(codes[j][bp][:].bitcast(I32))[:, :, dst],
                                      in_=rows_of(codes[1][bp][:].bitcast(I32))[:, :, src])

        accs = {}
        r_tiles = {}

        def mx_passes(s, half, i_list, first, last, lo=0, n=512):
            bp, hq = divmod(s, 4)
            if first and lo == 0:
                acc_new = accp.tile([P, 512], F32, name="acc", tag="acc")
                accs[(s, half)] = acc_new
            acc = accs[(s, half)]
            todo = [(i, j) for j in (1, 0, 2) for i in i_list]
            for m, (i, j) in enumerate(todo):
                blk = 2 * (3 * i + j) + half
                px = (ROWS * hq + i) * 64 + lo
                nc.tensor.matmul_mx(
                    out=acc[:, lo:lo + n],
                    lhsT=wc[:, blk * P:(blk + 1) * P].bitcast(FP8X4),
                    lhsT_scale=ws[:, blk * P:(blk + 1) * P],
                    rhs=codes[j][bp][:, px:px + n].bitcast(FP8X4),
                    rhs_scale=planes[j][bp][:, px:px + n],
                    start=(first and m == 0), stop=(last and m == len(todo) - 1),
                )

        def relu(s, half, eng, lo=0, n=512):
            if lo == 0:
                r_new = rpool.tile([P, 512], F32, name="r")
                r_tiles[(s, half)] = r_new
            dst, src = r_tiles[(s, half)][:, lo:lo + n], accs[(s, half)][:, lo:lo + n]
            if eng is nc.vector:
                nc.vector.tensor_scalar(out=dst, in0=src, scalar1=bias_sb[:, half:half + 1], scalar2=0.0,
                                        op0=ALU.add, op1=ALU.max)
            else:
                nc.scalar.activation(out=dst, in_=src, func=ACT.Relu, bias=bias_sb[:, half:half + 1], scale=1.0)

        r_banks = {}

        def r_words(s, pg, where=(tp, "tp")):
            pool, tag = where
            rt = pool.tile([P, 2, 2, P], F32, name="rt", tag=tag)
            for pl in range(2):
                pb = 2 * pg + pl
                for half in range(2):
                    nc.tensor.transpose(rt[:, pl, half, :], r_tiles[(s, half)][:, pb * P:(pb + 1) * P], ident_f[:])
            r_banks[(s, pg)] = rt

        def r_squares(s, pg):
            for pl in range(2):
                junk = junkp.tile([P, 2, P], BF16, name="junk2")
                col = out_col(s, 2 * pg + pl)
                nc.scalar.activation(out=junk[:], in_=r_banks[(s, pg)][:, pl], func=ACT.Square,
                                     accum_out=sm["m2"][:, col:col + 1])

        def out_pow(s, lo=0, n=4):
            lo = out_col(s, lo)
            nc.scalar.activation(out=cols("y2o", lo, n), in_=cols("m2", lo, n), func=ACT.Identity,
                                 bias=tiny[:, 1:2], scale=0.01)
            nc.gpsimd.tensor_tensor(out=cols("rzo", lo, n), in0=cols("y2o", lo, n), in1=mhalf8[:, 0:n], op=ALU.pow)

        def out_z(s, lo=0, n=4):
            lo = out_col(s, lo)
            nc.vector.tensor_tensor(out=cols("zm", lo, n), in0=cols("y2o", lo, n), in1=cols("rzo", lo, n), op=ALU.mult)

        def out_tanh(s, lo=0, n=4):
            lo = out_col(s, lo)
            nc.scalar.activation(out=cols("th", lo, n), in_=cols("zm", lo, n), func=ACT.Tanh)

        def out_t(s, lo=0, n=4):
            lo = out_col(s, lo)
            nc.vector.tensor_tensor(out=cols("tf", lo, n), in0=cols("th", lo, n), in1=cols("rzo", lo, n), op=ALU.mult)

        def out_scalar(s, lo=0, n=4):
            for dst, func, src in (("th", ACT.Tanh, "y2o"), ("tf", ACT.Copy, "th")):
                for k in range(lo, lo + n):
                    at = slice(out_col(s, k), out_col(s, k) + 1)
                    nc.scalar.activation(out=sm[dst][:, at], in_=sm[src][:, at], func=func, scale=sm["rzo"][:, at])

        t_banks = {}
        out_v = out.rearrange("b (p h) y x -> h b p y x", h=2)

        def t_bcast(s, lo=0, n=4):
            tb = bc.tile([P, 4, P], F32, name="tb", tag="bc")
            t_banks[(s, lo)] = tb
            for k in range(n):
                col = out_col(s, lo + k)
                nc.tensor.transpose(tb[:, k, :], sm["tf"][:, col:col + 1].to_broadcast([P, P]), ident_f[:])

        def finish(s, half, lo=0, n=4, queue=nc.sync):
            bp, hq = divmod(s, 4)
            rows = 2 * n
            tv = t_banks[(s, lo)][:, 0:n, :].rearrange("p k (a b w) -> p (k a) b w", a=2, b=2)
            ob = opool.tile([P, 2, rows, W], F32, name="ob%d" % rows)
            rv = r_tiles[(s, half)][:, lo * P:(lo + n) * P].rearrange("p (h b w) -> p h b w", h=rows, b=2)
            nc.vector.tensor_tensor(out=ob[:].rearrange("p b h w -> p h b w"), in0=rv, in1=tv, op=ALU.mult)
            r0 = ROWS * hq + 2 * lo
            queue.dma_start(
                out=out_v[half][2 * bp:2 * bp + 2, :, r0:r0 + rows, :].rearrange("b p h w -> p b (h w)"),
                in_=ob[:].rearrange("p b h w -> p b (h w)"),
            )

        bias_sb = const.tile([P, 2], F32, name="bias_sb")

        V, S = nc.vector, nc.scalar
        clear_borders(0)
        clear_borders(1)
        x_gram(0, 3)
        in_pow(0, V)
        x_words(1)
        x_squares(1, (0,))
        in_z2(0)
        in_zc(0)
        in_log(0)
        in_dd(0)
        in_gg(0)
        x_squares(1, (1,))
        in_pow(1, S)
        for k in (1, 0, 2):
            w_transpose(k, S)
        g_bcast(0)
        for k in (4, 3):
            w_transpose(k, S)
        u_mult(0, 0)
        in_z2(1)
        w_quant(1)
        in_zc(1)
        in_log(1)
        w_transpose(5, S)
        u_mult(0, 1)
        in_dd(1)
        w_quant(4)
        in_gg(1)
        u_quant(0)
        w_quant(0)
        u_move(0, 0, False)
        w_quant(3)
        u_move(0, 0, True)
        u_move(0, 2, False)
        w_quant(2)
        u_move(0, 2, True)
        w_quant(5)
        nc.vector.tensor_copy(out=bias_sb[:], in_=btile[:])
        x_words(2)
        x_squares(2)
        in_pow(2, S)
        g_bcast(1)

        def fin(s):
            finish(s, 0)
            finish(s, 1)

        def norm_in(n):
            x_words(n)
            x_squares(n)
            in_pow(n, S)

        def norm_out(s):
            for pg in range(2):
                r_words(s, pg)
                r_squares(s, pg)

        scaled = {3: (0,), 4: (1,), 5: (2, 3), 6: (4,)}
        for c in range(LAST):
            whole = c % 4 == 3
            taps = [0, 1, 2] if whole else [0, 1]
            if c == 1:
                mx_passes(c, 0, taps, True, whole)
            if c % 4 > 0:
                for half in range(2):
                    mx_passes(c - 1, half, [2], False, True)
                    relu(c - 1, half, S)
            if c > 3:
                out_scalar(c - 2)
            if c == 1:
                norm_in(5)
            if c == 2:
                x_squares(6)
                in_pow(6, S)
            if c != 1:
                mx_passes(c, 0, taps, True, whole)
            if whole:
                relu(c, 0, S)
            fins = [(s, half) for s in scaled.get(c - 1, ()) for half in range(2)]
            if c == 0:
                for k in (6, 7, 8):
                    w_transpose(k, S)
            u_mult(c + 1, 0)
            if c == 0:
                in_z2(2)
                in_zc(2)
                in_log(2)
                norm_in(3)
            if c == 1:
                in_dd(3)
            if c == 2:
                in_dd(4)
                in_z2(5)
            if c == 3:
                in_dd(6)
                in_z2(7)
            u_mult(c + 1, 1)
            if c == 0:
                in_dd(2)
            if c == 1:
                in_gg(3)
                in_z2(4)
            if c == 2:
                in_gg(4)
                in_zc(5)
                in_log(5)
            if c == 3:
                in_gg(6)
                in_zc(7)
                in_log(7)
                out_scalar(0)
                out_scalar(1)
            u_quant(c + 1)
            if c == 0:
                in_gg(2)
            if c == 1:
                in_zc(4)
                in_log(4)
            u_move(c + 1, 0, False)
            if c in (2, 3):
                in_dd({2: 5, 3: 7}[c])
            u_move(c + 1, 0, True)
            if c in (2, 3):
                in_gg({2: 5, 3: 7}[c])
            u_move(c + 1, 2, False)
            u_move(c + 1, 2, True)
            if c == 0:
                w_quant(6)
                in_z2(3)
                w_quant(7)
                in_zc(3)
                w_quant(8)
            if c == 2:
                in_z2(6)
            for s, half in fins:
                finish(s, half)
            mx_passes(c, 1, taps, True, whole)
            if whole:
                relu(c, 1, S)
            if c > 0:
                norm_out(c - 1)
            for n in {0: (2,), 1: (3,), 2: (4, 5), 3: (6,), 4: (7,)}.get(c, ()):
                g_bcast(n)
            for s in scaled.get(c, ()):
                t_bcast(s)
            if c > 0:
                out_pow(c - 1)
            if c < 2:
                x_words((4, 6)[c], (bc, "bc"))
            if c == 0:
                x_squares(4)
                in_pow(4, S)
            if c == 2:
                x_gram(7)
                in_pow(7, V)
                in_zc(6)
            if c in (0, 2):
                in_log({0: 3, 2: 6}[c])

        for half in range(2):
            mx_passes(6, half, [2], False, True)
            relu(6, half, S)
        out_scalar(5)
        for half in range(2):
            mx_passes(7, half, [0, 1, 2], True, True, 0, 256)
            relu(7, half, V, 0, 256)
        fin(4)
        norm_out(6)
        out_pow(6)
        t_bcast(5)
        r_words(7, 0, (accp, "acc"))
        r_squares(7, 0)
        out_pow(7, 0, 2)
        for half in range(2):
            mx_passes(7, half, [0, 1, 2], True, True, 256, 256)
        finish(5, 0)
        relu(7, 0, V, 256, 256)
        out_z(6)
        out_tanh(6)
        relu(7, 1, S, 256, 256)
        out_t(6)
        out_scalar(7, 0, 2)
        r_words(7, 1)
        r_squares(7, 1)
        out_pow(7, 2, 2)
        t_bcast(6)
        t_bcast(7, 0, 2)
        finish(5, 1)
        finish(6, 0)
        finish(6, 1)
        out_scalar(7, 2, 2)
        t_bcast(7, 2, 2)
        finish(7, 0, 0, 2)
        finish(7, 1, 0, 2)
        finish(7, 0, 2, 2)
        finish(7, 1, 2, 2, S)
